import numpy as np
import ml_dtypes


def mxq(x, axis, fmt="e4m3"):
    dtype, down = {"e4m3": (ml_dtypes.float8_e4m3fn, 7), "e5m2": (ml_dtypes.float8_e5m2, 14)}[fmt]
    v = np.moveaxis(np.asarray(x, np.float32).astype(ml_dtypes.bfloat16).astype(np.float64), axis, -1)
    blocks = v.reshape(v.shape[:-1] + (-1, 32))
    amax = np.abs(blocks).max(-1, keepdims=True)
    byte = np.maximum(np.where(amax > 0, np.frexp(amax)[1] - 1 + 127, 0) - down, 1)
    scale = np.exp2(byte - 127.0)
    codes = (blocks / scale).astype(np.float32).astype(dtype).astype(np.float64)
    return np.moveaxis((codes * scale).reshape(v.shape), -1, axis)


WIDE = False


def mx_kscale(k):
    if not WIDE:
        return np.ones(k)
    levels = np.array([10, -10, 5, -5, 0])
    a = np.random.permutation(np.resize(levels, k // 512 * 4)).reshape(k // 512, 4)
    idx = np.arange(k)
    return np.exp2(a[idx // 512, idx % 128 // 32])


BF16 = ml_dtypes.bfloat16


def bf(x):
    return np.asarray(x, np.float32).astype(BF16)


def f64(x):
    return np.asarray(x).astype(np.float64)


B, K, G, D, FF, F, P, H = 16, 64, 128, 1024, 2048, 2048, 7, 8
NC = K * G
EPS = 1e-5


def layernorm(x, g, b):
    m = x.mean(-1, keepdims=True)
    v = ((x - m) ** 2).mean(-1, keepdims=True)
    return (x - m) / np.sqrt(v + EPS) * g + b


def setup_inputs():
    n = np.random.standard_normal
    s, t = mx_kscale(FF), mx_kscale(D)
    return {
        "ff_hid": bf(np.maximum(n((B, K, FF)), 0.0) * s),
        "tgt": bf(n((B, K, D))),
        "w2": bf(n((FF, D)) / np.sqrt(FF) / s[:, None]),
        "b2": bf(0.1 * n(D)),
        "g3": bf((1.0 + 0.1 * n(D)) * t),
        "be3": bf(0.1 * n(D) * t),
        "dup_pool": bf(n((K, D, G)) / np.sqrt(D) / t[None, :, None]),
        "dup_bias": bf(0.2 * n(NC)),
    }


def reference(ff_hid, tgt, w2, b2, g3, be3, dup_pool, dup_bias):
    ff = (mxq(f64(ff_hid), 2, "e4m3") @ mxq(f64(w2), 0, "e4m3")) + f64(b2)
    h = layernorm(f64(tgt) + ff, f64(g3), f64(be3))
    out_extrap = (mxq(h, 2, "e4m3").transpose(1, 0, 2) @ mxq(f64(dup_pool), 1, "e4m3")).transpose(1, 0, 2)
    return out_extrap.reshape(B, -1)[:, :NC] + f64(dup_bias)

@@ -1,0 +1,288 @@
+from contextlib import ExitStack
+
+import concourse.mybir as mybir
+from concourse.masks import make_identity
+
+F32 = mybir.dt.float32
+BF16 = mybir.dt.bfloat16
+U32 = mybir.dt.uint32
+U8 = mybir.dt.uint8
+FP8X4 = mybir.dt.float8_e4m3fn_x4
+ALU = mybir.AluOpType
+ACT = mybir.ActivationFunctionType
+
+P = 128
+NB = 16
+NK = 64
+NG = 128
+D = 1024
+FF = 2048
+EPS = 1e-5
+FLOPS = 2 * NB * NK * FF * D + 2 * NB * NK * D * NG
+
+RAW_BUFS = 9
+V_BLOCKS = 4
+
+
+def regroup(nc, dst4, src4, v_blocks):
+    if v_blocks > 0:
+        nc.vector.tensor_copy(
+            out=dst4[:, 0:v_blocks].rearrange("p k (c i) t -> p k c t i", i=4),
+            in_=src4[:, 0:v_blocks].rearrange("p k t (c i) -> p k c t i", i=4),
+        )
+    for k in range(v_blocks, 8):
+        nc.scalar.copy(
+            out=dst4[:, k].rearrange("p (c i) t -> p c t i", i=4),
+            in_=src4[:, k].rearrange("p t (c i) -> p c t i", i=4),
+        )
+
+
+def tile_mldecoder_pb_kernel(tc, ff_hid, tgt, w2, b2, g3, be3, dup_pool, dup_bias, out):
+    nc = tc.nc
+    ffv = ff_hid.rearrange("b (kk i) f -> (b kk) i f", i=8)
+    tgv = tgt.rearrange("b (kk i) d -> (b kk) i d", i=8)
+    w2v = w2.rearrange("(g u q e) n -> g q u (e n)", g=4, u=2, e=2)
+    dv = dup_pool.rearrange("(kk i) (c p j) g -> i c p kk (j g)", i=8, c=2, j=4)
+    outv = out.rearrange("b (kk x) -> (b kk) x", kk=8)
+
+    with ExitStack() as ctx:
+        const = ctx.enter_context(tc.tile_pool(name="const", bufs=1))
+        keep = ctx.enter_context(tc.tile_pool(name="keep", bufs=1))
+        rawp = ctx.enter_context(tc.tile_pool(name="rawp", bufs=RAW_BUFS))
+        grpp = ctx.enter_context(tc.tile_pool(name="grpp", bufs=3))
+        xp = ctx.enter_context(tc.tile_pool(name="xp", bufs=4))
+        work2 = ctx.enter_context(tc.tile_pool(name="work2", bufs=2))
+        work4 = ctx.enter_context(tc.tile_pool(name="work4", bufs=4))
+        small = ctx.enter_context(tc.tile_pool(name="small", bufs=4))
+        psum = ctx.enter_context(tc.psum_pool(name="psum", bufs=2))
+
+        fraws = []
+        wraws = []
+        traws = []
+        xraws = {}
+
+        def load_ff(j):
+            fraw = rawp.tile([P, 2, FF], BF16, tag="raw")
+            nc.sync.dma_start(out=fraw[:], in_=ffv[:, 2 * j:2 * j + 2, :])
+            fraws.append(fraw)
+
+        def load_w2(g):
+            wraw = rawp.tile([P, 4, D], BF16, tag="raw")
+            nc.sync.dma_start(out=wraw[:].rearrange("p (u e) n -> p u (e n)", u=2), in_=w2v[g])
+            wraws.append(wraw)
+
+        def load_tgt(a):
+            traw = rawp.tile([P, 4, D], BF16, tag="raw")
+            nc.sync.dma_start(out=traw[:], in_=tgv[:, 4 * a:4 * a + 4, :])
+            traws.append(traw)
+
+        def load_x(i, c):
+            xraw = rawp.tile([P, 8, 512], BF16, tag="raw")
+            nc.sync.dma_start(out=xraw[:], in_=dv[i, c])
+            xraws[(i, c)] = xraw
+
+        b2bc = const.tile([P, D], BF16)
+        nc.scalar.dma_start(out=b2bc[:], in_=b2.partition_broadcast(P))
+        g3r = const.tile([P, 2, 4], BF16)
+        nc.scalar.dma_start(out=g3r[:], in_=g3.rearrange("(c p t) -> p c t", c=2, t=4))
+        be3r = const.tile([P, 2, 4], BF16)
+        nc.scalar.dma_start(out=be3r[:], in_=be3.rearrange("(c p t) -> p c t", c=2, t=4))
+        braw = const.tile([P, P], BF16)
+        nc.vector.memset(braw[:], 0.0)
+        nc.scalar.dma_start(out=braw[0:NK, :], in_=dup_bias.rearrange("(k g) -> k g", g=NG))
+
+        load_w2(0)
+        load_ff(0)
+        for g in range(1, 4):
+            load_w2(g)
+        load_tgt(0)
+        for j in range(1, 4):
+            load_ff(j)
+        load_tgt(1)
+        for i in range(8):
+            for c in range(2):
+                load_x(i, c)
+
+        eps = const.tile([P, 1], F32)
+        nc.vector.memset(eps[:], EPS)
+        warm = const.tile([P, 1], F32)
+        nc.scalar.activation(out=warm[:], in_=eps[:], func=ACT.Sqrt)
+
+        ident = const.tile([P, P], F32)
+        make_identity(nc, ident[:])
+        identb = const.tile([P, P], BF16)
+        make_identity(nc, identb[:])
+        perm = const.tile([P, P], F32)
+        nc.vector.tensor_copy(
+            out=perm[:].rearrange("p (k b) -> p k b", k=8),
+            in_=ident[:].rearrange("p (b k) -> p k b", k=8),
+        )
+        g3T = const.tile([P, 8], F32)
+        nc.vector.tensor_copy(out=g3T[:], in_=g3r[:].rearrange("p c t -> p (c t)"))
+        be3T = const.tile([P, 8], F32)
+        nc.vector.tensor_copy(out=be3T[:], in_=be3r[:].rearrange("p c t -> p (c t)"))
+        o_all = const.tile([P, D], F32)
+
+        w2c = keep.tile([P, 4, D], U32, align_bytes=64)
+        w2s = keep.tile([P, 4, D], U8, align_bytes=64)
+        fc = keep.tile([P, 4, 1024], U32, align_bytes=64)
+        fs = keep.tile([P, 4, 1024], U8, align_bytes=64)
+        hc = keep.tile([P, 4, 512], U32, align_bytes=64)
+        hs = keep.tile([P, 4, 512], U8, align_bytes=64)
+
+        def prep_ff(j):
+            fraw = fraws[j]
+            grp = grpp.tile([P, 4096], BF16, tag="grp", align_bytes=64)
+            gw = grp[:].bitcast(F32).rearrange("p (i g r u) -> p i g r u", i=2, g=4, u=2)
+            for i2 in range(2):
+                words = fraw[:, i2, :].bitcast(F32)
+                for gp in range(2):
+                    tp = psum.tile([P, 2, 2, P], F32, tag="tp")
+                    for gq in range(2):
+                        for u in range(2):
+                            col = 256 * (2 * gp + gq) + 128 * u
+                            nc.tensor.transpose(tp[:, gq, u, :], words[:, col:col + 128], ident[:])
+                    nc.scalar.copy(out=gw[:, i2, 2 * gp:2 * gp + 2], in_=tp[:].rearrange("p g u r -> p g r u"))
+            nc.vector.quantize_mx(out=fc[:, j, :].bitcast(FP8X4), scales=fs[:, j, :], in_=grp[:])
+
+        def prep_w2(g):
+            grp = grpp.tile([P, 4096], BF16, tag="grp", align_bytes=64)
+            regroup(
+                nc,
+                grp[:].rearrange("p (k n t) -> p k n t", k=8, t=4),
+                wraws[g][:].rearrange("p t (k n) -> p k t n", k=8),
+                V_BLOCKS,
+            )
+            nc.vector.quantize_mx(out=w2c[:, g, :].bitcast(FP8X4), scales=w2s[:, g, :], in_=grp[:])
+
+        def stage1(i):
+            j = i // 2
+            i2 = i % 2
+            tgtb = work2.tile([P, D], F32, tag="tgtb")
+            nc.vector.tensor_tensor(out=tgtb[:], in0=traws[i // 4][:, i % 4, :], in1=b2bc[:], op=ALU.add)
+            u = work2.tile([P, D], F32, tag="u")
+            ssum = small.tile([P, 2], F32, tag="ssum")
+            for h in range(2):
+                mm = psum.tile([P, 512], F32, tag="mm")
+                for g in range(4):
+                    off = (i2 * 4 + g) * 128
+                    nc.tensor.matmul_mx(
+                        out=mm[:],
+                        lhsT=fc[:, j, off:off + 128].bitcast(FP8X4),
+                        lhsT_scale=fs[:, j, off:off + 128],
+                        rhs=w2c[:, g, 512 * h:512 * h + 512].bitcast(FP8X4),
+                        rhs_scale=w2s[:, g, 512 * h:512 * h + 512],
+                        start=(g == 0),
+                        stop=(g == 3),
+                    )
+                nc.vector.scalar_tensor_tensor(
+                    out=u[:, 512 * h:512 * h + 512],
+                    in0=mm[:],
+                    scalar=0.0,
+                    in1=tgtb[:, 512 * h:512 * h + 512],
+                    op0=ALU.add,
+                    op1=ALU.add,
+                    accum_out=ssum[:, h:h + 1],
+                )
+            negmean = small.tile([P, 1], F32, tag="negmean")
+            nc.vector.tensor_scalar(
+                out=negmean[:], in0=ssum[:, 0:1], scalar1=ssum[:, 1:2], scalar2=-1.0 / D,
+                op0=ALU.add, op1=ALU.mult,
+            )
+            sq = work2.tile([P, D], BF16, tag="sq")
+            ssq = small.tile([P, 1], F32, tag="ssq")
+            nc.scalar.activation(out=sq[:], in_=u[:], func=ACT.Square, bias=negmean[:], scale=1.0, accum_out=ssq[:])
+            std = small.tile([P, 1], F32, tag="std")
+            nc.scalar.activation(out=std[:], in_=ssq[:], func=ACT.Sqrt, bias=eps[:], scale=1.0 / D)
+            rstd = small.tile([P, 1], F32, tag="rstd")
+            nc.vector.reciprocal(out=rstd[:], in_=std[:])
+            nbias = small.tile([P, 1], F32, tag="nbias")
+            nc.vector.tensor_tensor(out=nbias[:], in0=negmean[:], in1=rstd[:], op=ALU.mult)
+            zp = work4.tile([P, D], F32, tag="zp")
+            nc.scalar.activation(
+                out=zp[:].rearrange("p (c t m) -> p c m t", c=2, t=4),
+                in_=u[:].rearrange("p (c m t) -> p c m t", c=2, t=4),
+                func=ACT.Identity, bias=nbias[:], scale=rstd[:],
+            )
+            return zp
+
+        def flip_h(j, zps):
+            hTp = work2.tile([P, 8, 256], BF16, tag="hTp")
+            for pq in range(4):
+                zt = psum.tile([P, 2, 2, P], F32, tag="zt")
+                for q in range(2):
+                    pl = 2 * pq + q
+                    for i2 in range(2):
+                        nc.tensor.transpose(zt[:, q, i2, :], zps[i2][:, pl * 128:(pl + 1) * 128], perm[:])
+                for q in range(2):
+                    pl = 2 * pq + q
+                    nc.scalar.activation(
+                        out=hTp[:, pl, :], in_=zt[:, q].rearrange("p i r -> p (i r)"),
+                        func=ACT.Identity, bias=be3T[:, pl:pl + 1], scale=g3T[:, pl:pl + 1],
+                    )
+            hg = work2.tile([P, 2048], BF16, tag="hg", align_bytes=64)
+            nc.vector.tensor_copy(
+                out=hg[:].rearrange("p (c a i t) -> p c a t i", c=2, i=4, t=4),
+                in_=hTp[:].rearrange("p (c t) (a i) -> p c a t i", c=2, i=4),
+            )
+            nc.vector.quantize_mx(out=hc[:, j, :].bitcast(FP8X4), scales=hs[:, j, :], in_=hg[:])
+
+        def prep_x(i, c):
+            grp = grpp.tile([P, 4096], BF16, tag="grp", align_bytes=64)
+            regroup(
+                nc,
+                grp[:].rearrange("p (k n t) -> p k n t", k=8, t=4),
+                xraws[(i, c)][:].rearrange("p k (t n) -> p k t n", t=4),
+                V_BLOCKS,
+            )
+            xc = xp.tile([P, 1024], U32, tag="xc", align_bytes=64)
+            xs = xp.tile([P, 1024], U8, tag="xs", align_bytes=64)
+            nc.vector.quantize_mx(out=xc[:].bitcast(FP8X4), scales=xs[:], in_=grp[:])
+            return (xc, xs)
+
+        def stage2(i, xq):
+            j = i // 2
+            i2 = i % 2
+            oT = work2.tile([P, P], F32, tag="oT")
+            for hh in range(2):
+                s2 = psum.tile([P, 512], F32, tag="s2")
+                for kq in range(4):
+                    kk = 4 * hh + kq
+                    for c in range(2):
+                        off = (c * 2 + i2) * 128
+                        nc.tensor.matmul_mx(
+                            out=s2[:, kq * 128:(kq + 1) * 128],
+                            lhsT=xq[c][0][:, kk * 128:(kk + 1) * 128].bitcast(FP8X4),
+                            lhsT_scale=xq[c][1][:, kk * 128:(kk + 1) * 128],
+                            rhs=hc[:, j, off:off + 128].bitcast(FP8X4),
+                            rhs_scale=hs[:, j, off:off + 128],
+                            start=(c == 0),
+                            stop=(c == 1),
+                        )
+                nc.vector.tensor_tensor(
+                    out=oT[:].rearrange("p (b k) -> p b k", k=8)[:, :, 4 * hh:4 * hh + 4],
+                    in0=s2[:].rearrange("p (x y) -> p x y", y=16)[:, 4 * hh:4 * hh + 28:9, :].rearrange("p q b -> p b q"),
+                    in1=biasT[:, 0:NK].rearrange("p (k i) -> p i k", i=8)[:, i:i + 1, 4 * hh:4 * hh + 4].to_broadcast([P, NB, 4]),
+                    op=ALU.add,
+                )
+            ot = psum.tile([P, P], F32, tag="tp")
+            nc.tensor.transpose(ot[:], oT[:], ident[:])
+            nc.scalar.copy(out=o_all[:, i * 128:(i + 1) * 128], in_=ot[:])
+            nc.scalar.dma_start(out=outv[:, i * 128:(i + 1) * 128], in_=o_all[:, i * 128:(i + 1) * 128])
+
+        prep_w2(0)
+        prep_ff(0)
+        for g in range(1, 4):
+            prep_w2(g)
+        for j in range(4):
+            if j > 0:
+                prep_ff(j)
+            zps = [stage1(2 * j), stage1(2 * j + 1)]
+            flip_h(j, zps)
+        bps = psum.tile([P, P], BF16, tag="tp")
+        nc.tensor.transpose(bps[:], braw[:], identb[:])
+        biasT = const.tile([P, P], F32)
+        nc.vector.tensor_copy(out=biasT[:], in_=bps[:])
+        for i in range(8):
+            xq = [prep_x(i, 0), prep_x(i, 1)]
+            stage2(i, xq)

@@ -17,24 +17,38 @@ NK = 64
 NG = 128
 D = 1024
 FF = 2048
+NT = 8
 EPS = 1e-5
 FLOPS = 2 * NB * NK * FF * D + 2 * NB * NK * D * NG
 
-RAW_BUFS = 9
 V_BLOCKS = 4
+S_FIRST = 1
+LAG = {"FT": 0, "FE": 2, "FQ": 3, "T": 3, "MM": 5, "E": 7, "SQ": 8, "R": 8, "ZE": 11, "HR": 11, "HQ": 12, "O2": 14, "OE": 3, "OC": 7}
+SPARSE_UNTIL = 18
+PRE_BULK = 4
+PRE_F = 2
+PRE_T = 4
+CONST_TICK = 6
 
 
-def regroup(nc, dst4, src4, v_blocks):
-    if v_blocks > 0:
-        nc.vector.tensor_copy(
-            out=dst4[:, 0:v_blocks].rearrange("p k (c i) t -> p k c t i", i=4),
-            in_=src4[:, 0:v_blocks].rearrange("p k t (c i) -> p k c t i", i=4),
-        )
-    for k in range(v_blocks, 8):
-        nc.scalar.copy(
-            out=dst4[:, k].rearrange("p (c i) t -> p c t i", i=4),
-            in_=src4[:, k].rearrange("p t (c i) -> p c t i", i=4),
-        )
+def bulk_plan():
+    plan = [("w", g) for g in range(4)]
+    s = 0
+    while s < 16:
+        m = len(plan)
+        if m < SPARSE_UNTIL and m % 2 == 0:
+            plan.append(None)
+        else:
+            plan.append(("x", s))
+            s += 1
+    return plan
+
+
+def tile_at(m, lag):
+    t = m - lag
+    if t >= 0 and t % 2 == 0 and t // 2 < NT:
+        return t // 2
+    return -1
 
 
 def tile_mldecoder_pb_kernel(tc, ff_hid, tgt, w2, b2, g3, be3, dup_pool, dup_bias, out):
@@ -44,42 +58,27 @@ def tile_mldecoder_pb_kernel(tc, ff_hid, tgt, w2, b2, g3, be3, dup_pool, dup_bia
     w2v = w2.rearrange("(g u q e) n -> g q u (e n)", g=4, u=2, e=2)
     dv = dup_pool.rearrange("(kk i) (c p j) g -> i c p kk (j g)", i=8, c=2, j=4)
     outv = out.rearrange("b (kk x) -> (b kk) x", kk=8)
+    plan = bulk_plan()
+    q_tick = {}
+    for m in range(len(plan)):
+        if plan[m] is not None:
+            q_tick[plan[m]] = m + 1
+    o_tick = [max(2 * i + LAG["O2"], q_tick[("x", 2 * i + 1)] + 1) for i in range(NT)]
+    n_ticks = max(o_tick) + LAG["OC"] + 1
 
     with ExitStack() as ctx:
         const = ctx.enter_context(tc.tile_pool(name="const", bufs=1))
         keep = ctx.enter_context(tc.tile_pool(name="keep", bufs=1))
-        rawp = ctx.enter_context(tc.tile_pool(name="rawp", bufs=RAW_BUFS))
+        rawp = ctx.enter_context(tc.tile_pool(name="rawp", bufs=6))
+        frawp = ctx.enter_context(tc.tile_pool(name="frawp", bufs=3))
         grpp = ctx.enter_context(tc.tile_pool(name="grpp", bufs=3))
-        xp = ctx.enter_context(tc.tile_pool(name="xp", bufs=4))
+        xp = ctx.enter_context(tc.tile_pool(name="xp", bufs=5))
+        work1 = ctx.enter_context(tc.tile_pool(name="work1", bufs=1))
         work2 = ctx.enter_context(tc.tile_pool(name="work2", bufs=2))
         work4 = ctx.enter_context(tc.tile_pool(name="work4", bufs=4))
         small = ctx.enter_context(tc.tile_pool(name="small", bufs=4))
         psum = ctx.enter_context(tc.psum_pool(name="psum", bufs=2))
-
-        fraws = []
-        wraws = []
-        traws = []
-        xraws = {}
-
-        def load_ff(j):
-            fraw = rawp.tile([P, 2, FF], BF16, tag="raw")
-            nc.sync.dma_start(out=fraw[:], in_=ffv[:, 2 * j:2 * j + 2, :])
-            fraws.append(fraw)
-
-        def load_w2(g):
-            wraw = rawp.tile([P, 4, D], BF16, tag="raw")
-            nc.sync.dma_start(out=wraw[:].rearrange("p (u e) n -> p u (e n)", u=2), in_=w2v[g])
-            wraws.append(wraw)
-
-        def load_tgt(a):
-            traw = rawp.tile([P, 4, D], BF16, tag="raw")
-            nc.sync.dma_start(out=traw[:], in_=tgv[:, 4 * a:4 * a + 4, :])
-            traws.append(traw)
-
-        def load_x(i, c):
-            xraw = rawp.tile([P, 8, 512], BF16, tag="raw")
-            nc.sync.dma_start(out=xraw[:], in_=dv[i, c])
-            xraws[(i, c)] = xraw
+        ctx.enter_context(tc.manual_schedule())
 
         b2bc = const.tile([P, D], BF16)
         nc.scalar.dma_start(out=b2bc[:], in_=b2.partition_broadcast(P))
@@ -91,23 +90,39 @@ def tile_mldecoder_pb_kernel(tc, ff_hid, tgt, w2, b2, g3, be3, dup_pool, dup_bia
         nc.vector.memset(braw[:], 0.0)
         nc.scalar.dma_start(out=braw[0:NK, :], in_=dup_bias.rearrange("(k g) -> k g", g=NG))
 
-        load_w2(0)
-        load_ff(0)
-        for g in range(1, 4):
-            load_w2(g)
-        load_tgt(0)
-        for j in range(1, 4):
-            load_ff(j)
-        load_tgt(1)
-        for i in range(8):
-            for c in range(2):
-                load_x(i, c)
+        wanted = []
+        for m in range(len(plan)):
+            if plan[m] is not None:
+                wanted.append((m - PRE_BULK, plan[m]))
+        for t in range(NT):
+            wanted.append((2 * t + LAG["FT"] - PRE_F, ("f", t)))
+            if t % 2 == 0:
+                wanted.append((2 * t + LAG["T"] - PRE_T, ("t", t // 2)))
+        raws = {}
+        for item in sorted(wanted, key=lambda pair: pair[0]):
+            kind = item[1][0]
+            idx = item[1][1]
+            if kind == "w":
+                wraw = rawp.tile([P, 4, D], BF16, tag="raw")
+                nc.sync.dma_start(out=wraw[:].rearrange("p (u e) n -> p u (e n)", u=2), in_=w2v[idx])
+                raws[item[1]] = wraw[:].rearrange("p t (k n) -> p k t n", k=8)
+            elif kind == "x":
+                xraw = rawp.tile([P, 8, 512], BF16, tag="raw")
+                nc.sync.dma_start(out=xraw[:], in_=dv[idx // 2, idx % 2])
+                raws[item[1]] = xraw[:].rearrange("p k (t n) -> p k t n", t=4)
+            elif kind == "f":
+                fraw = frawp.tile([P, FF], BF16, tag="fraw")
+                nc.sync.dma_start(out=fraw[:], in_=ffv[:, idx, :])
+                raws[item[1]] = fraw
+            else:
+                traw = work2.tile([P, 2, D], BF16, tag="traw")
+                nc.sync.dma_start(out=traw[:], in_=tgv[:, 2 * idx:2 * idx + 2, :])
+                raws[item[1]] = traw
 
         eps = const.tile([P, 1], F32)
         nc.vector.memset(eps[:], EPS)
         warm = const.tile([P, 1], F32)
         nc.scalar.activation(out=warm[:], in_=eps[:], func=ACT.Sqrt)
-
         ident = const.tile([P, P], F32)
         make_identity(nc, ident[:])
         identb = const.tile([P, P], BF16)
@@ -118,68 +133,115 @@ def tile_mldecoder_pb_kernel(tc, ff_hid, tgt, w2, b2, g3, be3, dup_pool, dup_bia
             in_=ident[:].rearrange("p (b k) -> p k b", k=8),
         )
         g3T = const.tile([P, 8], F32)
-        nc.vector.tensor_copy(out=g3T[:], in_=g3r[:].rearrange("p c t -> p (c t)"))
         be3T = const.tile([P, 8], F32)
-        nc.vector.tensor_copy(out=be3T[:], in_=be3r[:].rearrange("p c t -> p (c t)"))
+        bexp = const.tile([P, NT, P], F32)
         o_all = const.tile([P, D], F32)
 
         w2c = keep.tile([P, 4, D], U32, align_bytes=64)
         w2s = keep.tile([P, 4, D], U8, align_bytes=64)
-        fc = keep.tile([P, 4, 1024], U32, align_bytes=64)
-        fs = keep.tile([P, 4, 1024], U8, align_bytes=64)
-        hc = keep.tile([P, 4, 512], U32, align_bytes=64)
-        hs = keep.tile([P, 4, 512], U8, align_bytes=64)
+        fc = keep.tile([P, NT, 512], U32, align_bytes=64)
+        fs = keep.tile([P, NT, 512], U8, align_bytes=64)
+        hc = keep.tile([P, NT, 256], U32, align_bytes=64)
+        hs = keep.tile([P, NT, 256], U8, align_bytes=64)
 
-        def prep_ff(j):
-            fraw = fraws[j]
-            grp = grpp.tile([P, 4096], BF16, tag="grp", align_bytes=64)
-            gw = grp[:].bitcast(F32).rearrange("p (i g r u) -> p i g r u", i=2, g=4, u=2)
-            for i2 in range(2):
-                words = fraw[:, i2, :].bitcast(F32)
-                for gp in range(2):
-                    tp = psum.tile([P, 2, 2, P], F32, tag="tp")
-                    for gq in range(2):
-                        for u in range(2):
-                            col = 256 * (2 * gp + gq) + 128 * u
-                            nc.tensor.transpose(tp[:, gq, u, :], words[:, col:col + 128], ident[:])
-                    nc.scalar.copy(out=gw[:, i2, 2 * gp:2 * gp + 2], in_=tp[:].rearrange("p g u r -> p g r u"))
-            nc.vector.quantize_mx(out=fc[:, j, :].bitcast(FP8X4), scales=fs[:, j, :], in_=grp[:])
+        live = {}
 
-        def prep_w2(g):
-            grp = grpp.tile([P, 4096], BF16, tag="grp", align_bytes=64)
-            regroup(
-                nc,
-                grp[:].rearrange("p (k n t) -> p k n t", k=8, t=4),
-                wraws[g][:].rearrange("p t (k n) -> p k t n", k=8),
-                V_BLOCKS,
+        def consts():
+            nc.vector.tensor_copy(out=g3T[:], in_=g3r[:].rearrange("p c t -> p (c t)"))
+            nc.vector.tensor_copy(out=be3T[:], in_=be3r[:].rearrange("p c t -> p (c t)"))
+            bps = psum.tile([P, P], BF16, tag="s2")
+            nc.tensor.transpose(bps[:], braw[:], identb[:])
+            nc.vector.tensor_copy(
+                out=bexp[:].rearrange("p i (b k) -> p i b k", k=8),
+                in_=bps[:, 0:NK].rearrange("p (k i) -> p i k", i=8).unsqueeze(2).to_broadcast([P, NT, NB, 8]),
             )
-            nc.vector.quantize_mx(out=w2c[:, g, :].bitcast(FP8X4), scales=w2s[:, g, :], in_=grp[:])
 
-        def stage1(i):
-            j = i // 2
-            i2 = i % 2
+        def grp_of(key):
+            if ("g", key) not in live:
+                grp = grpp.tile([P, 4096], BF16, tag="grp", align_bytes=64)
+                live[("g", key)] = grp
+            return live[("g", key)]
+
+        def regroup_s(key, lo, hi):
+            dst4 = grp_of(key)[:].rearrange("p (k n t) -> p k n t", k=8, t=4)
+            for k in range(lo, hi):
+                nc.scalar.copy(
+                    out=dst4[:, k].rearrange("p (c i) t -> p c t i", i=4),
+                    in_=raws[key][:, k].rearrange("p t (c i) -> p c t i", i=4),
+                )
+
+        def regroup_v(key, nb):
+            dst4 = grp_of(key)[:].rearrange("p (k n t) -> p k n t", k=8, t=4)
+            nc.vector.tensor_copy(
+                out=dst4[:, 0:nb].rearrange("p k (c i) t -> p k c t i", i=4),
+                in_=raws[key][:, 0:nb].rearrange("p k t (c i) -> p k c t i", i=4),
+            )
+
+        def quantise_bulk(key):
+            grp = grp_of(key)
+            if key[0] == "w":
+                g = key[1]
+                nc.vector.quantize_mx(out=w2c[:, g, :].bitcast(FP8X4), scales=w2s[:, g, :], in_=grp[:])
+            else:
+                xc = xp.tile([P, 1024], U32, tag="xc", align_bytes=64)
+                xs = xp.tile([P, 1024], U8, tag="xs", align_bytes=64)
+                nc.vector.quantize_mx(out=xc[:].bitcast(FP8X4), scales=xs[:], in_=grp[:])
+                live[("c", key[1])] = (xc, xs)
+
+        def ff_transpose(t):
+            words = raws[("f", t)][:].bitcast(F32)
+            banks = []
+            for gp in range(2):
+                tp = psum.tile([P, 2, 2, P], F32, tag="tp")
+                for gq in range(2):
+                    for u in range(2):
+                        col = 256 * (2 * gp + gq) + 128 * u
+                        nc.tensor.transpose(tp[:, gq, u, :], words[:, col:col + 128], ident[:])
+                banks.append(tp)
+            live[("ftp", t)] = banks
+
+        def ff_out(t):
+            fg = work2.tile([P, 2048], BF16, tag="fg", align_bytes=64)
+            gw = fg[:].bitcast(F32).rearrange("p (g r u) -> p g r u", g=4, u=2)
+            for gp in range(2):
+                nc.scalar.copy(out=gw[:, 2 * gp:2 * gp + 2], in_=live[("ftp", t)][gp][:].rearrange("p g u r -> p g r u"))
+            live[("fg", t)] = fg
+
+        def ff_quantise(t):
+            nc.vector.quantize_mx(out=fc[:, t, :].bitcast(FP8X4), scales=fs[:, t, :], in_=live[("fg", t)][:])
+
+        def residual(t):
             tgtb = work2.tile([P, D], F32, tag="tgtb")
-            nc.vector.tensor_tensor(out=tgtb[:], in0=traws[i // 4][:, i % 4, :], in1=b2bc[:], op=ALU.add)
-            u = work2.tile([P, D], F32, tag="u")
-            ssum = small.tile([P, 2], F32, tag="ssum")
+            nc.vector.tensor_tensor(out=tgtb[:], in0=raws[("t", t // 2)][:, t % 2, :], in1=b2bc[:], op=ALU.add)
+            live[("tgtb", t)] = tgtb
+
+        def stage1_mm(t):
+            banks = []
             for h in range(2):
                 mm = psum.tile([P, 512], F32, tag="mm")
                 for g in range(4):
-                    off = (i2 * 4 + g) * 128
                     nc.tensor.matmul_mx(
                         out=mm[:],
-                        lhsT=fc[:, j, off:off + 128].bitcast(FP8X4),
-                        lhsT_scale=fs[:, j, off:off + 128],
+                        lhsT=fc[:, t, g * 128:(g + 1) * 128].bitcast(FP8X4),
+                        lhsT_scale=fs[:, t, g * 128:(g + 1) * 128],
                         rhs=w2c[:, g, 512 * h:512 * h + 512].bitcast(FP8X4),
                         rhs_scale=w2s[:, g, 512 * h:512 * h + 512],
                         start=(g == 0),
                         stop=(g == 3),
                     )
+                banks.append(mm)
+            live[("mm", t)] = banks
+
+        def stage1_out(t):
+            u = work4.tile([P, D], F32, tag="u")
+            ssum = small.tile([P, 2], F32, tag="ssum")
+            tgtb = live[("tgtb", t)]
+            for h in range(2):
                 nc.vector.scalar_tensor_tensor(
-                    out=u[:, 512 * h:512 * h + 512],
-                    in0=mm[:],
+                    out=u[:, 512 * h:512 * h + 512].rearrange("p (t m) -> p m t", t=4),
+                    in0=live[("mm", t)][h][:].rearrange("p (m t) -> p m t", t=4),
                     scalar=0.0,
-                    in1=tgtb[:, 512 * h:512 * h + 512],
+                    in1=tgtb[:, 512 * h:512 * h + 512].rearrange("p (m t) -> p m t", t=4),
                     op0=ALU.add,
                     op1=ALU.add,
                     accum_out=ssum[:, h:h + 1],
@@ -189,100 +251,145 @@ def tile_mldecoder_pb_kernel(tc, ff_hid, tgt, w2, b2, g3, be3, dup_pool, dup_bia
                 out=negmean[:], in0=ssum[:, 0:1], scalar1=ssum[:, 1:2], scalar2=-1.0 / D,
                 op0=ALU.add, op1=ALU.mult,
             )
-            sq = work2.tile([P, D], BF16, tag="sq")
+            live[("u", t)] = u
+            live[("negmean", t)] = negmean
+
+        def variance(t):
+            sq = work1.tile([P, D], BF16, tag="sq")
             ssq = small.tile([P, 1], F32, tag="ssq")
-            nc.scalar.activation(out=sq[:], in_=u[:], func=ACT.Square, bias=negmean[:], scale=1.0, accum_out=ssq[:])
+            nc.scalar.activation(
+                out=sq[:], in_=live[("u", t)][:], func=ACT.Square, bias=live[("negmean", t)][:], scale=1.0,
+                accum_out=ssq[:],
+            )
             std = small.tile([P, 1], F32, tag="std")
             nc.scalar.activation(out=std[:], in_=ssq[:], func=ACT.Sqrt, bias=eps[:], scale=1.0 / D)
-            rstd = small.tile([P, 1], F32, tag="rstd")
-            nc.vector.reciprocal(out=rstd[:], in_=std[:])
-            nbias = small.tile([P, 1], F32, tag="nbias")
-            nc.vector.tensor_tensor(out=nbias[:], in0=negmean[:], in1=rstd[:], op=ALU.mult)
-            zp = work4.tile([P, D], F32, tag="zp")
-            nc.scalar.activation(
-                out=zp[:].rearrange("p (c t m) -> p c m t", c=2, t=4),
-                in_=u[:].rearrange("p (c m t) -> p c m t", c=2, t=4),
-                func=ACT.Identity, bias=nbias[:], scale=rstd[:],
-            )
-            return zp
+            live[("std", t)] = std
 
-        def flip_h(j, zps):
-            hTp = work2.tile([P, 8, 256], BF16, tag="hTp")
-            for pq in range(4):
-                zt = psum.tile([P, 2, 2, P], F32, tag="zt")
-                for q in range(2):
-                    pl = 2 * pq + q
-                    for i2 in range(2):
-                        nc.tensor.transpose(zt[:, q, i2, :], zps[i2][:, pl * 128:(pl + 1) * 128], perm[:])
-                for q in range(2):
-                    pl = 2 * pq + q
-                    nc.scalar.activation(
-                        out=hTp[:, pl, :], in_=zt[:, q].rearrange("p i r -> p (i r)"),
-                        func=ACT.Identity, bias=be3T[:, pl:pl + 1], scale=g3T[:, pl:pl + 1],
+        def norm_factors(t):
+            rstd = small.tile([P, 1], F32, tag="rstd")
+            nc.vector.reciprocal(out=rstd[:], in_=live[("std", t)][:])
+            nbias = small.tile([P, 1], F32, tag="nbias")
+            nc.vector.tensor_tensor(out=nbias[:], in0=live[("negmean", t)][:], in1=rstd[:], op=ALU.mult)
+            dg = work4.tile([P, P], F32, tag="dg")
+            nc.vector.tensor_scalar_mul(out=dg[:], in0=perm[:], scalar1=rstd[:, 0:1])
+            live[("nbias", t)] = nbias
+            live[("dg", t)] = dg
+
+        def norm_flip(t):
+            banks = []
+            for bk in range(2):
+                zt = psum.tile([P, 4, P], F32, tag="zt")
+                for q in range(4):
+                    pl = 4 * bk + q
+                    nc.tensor.matmul(
+                        out=zt[:, q, :], lhsT=live[("u", t)][:, pl * 128:(pl + 1) * 128], rhs=live[("dg", t)][:],
+                        start=True, stop=False,
                     )
-            hg = work2.tile([P, 2048], BF16, tag="hg", align_bytes=64)
+                    nc.tensor.matmul(
+                        out=zt[:, q, :], lhsT=live[("nbias", t)][:, 0:1].to_broadcast([P, P]), rhs=perm[:],
+                        is_transpose=True, start=False, stop=True,
+                    )
+                banks.append(zt)
+            live[("zt", t)] = banks
+
+        def gain_shift(t):
+            hTp = work2.tile([P, 8, P], BF16, tag="hTp")
+            for pl in range(8):
+                nc.scalar.activation(
+                    out=hTp[:, pl, :], in_=live[("zt", t)][pl // 4][:, pl % 4, :],
+                    func=ACT.Identity, bias=be3T[:, pl:pl + 1], scale=g3T[:, pl:pl + 1],
+                )
+            live[("hTp", t)] = hTp
+
+        def h_regroup(t):
+            hg = work2.tile([P, 1024], BF16, tag="hg", align_bytes=64)
             nc.vector.tensor_copy(
                 out=hg[:].rearrange("p (c a i t) -> p c a t i", c=2, i=4, t=4),
-                in_=hTp[:].rearrange("p (c t) (a i) -> p c a t i", c=2, i=4),
+                in_=live[("hTp", t)][:].rearrange("p (c t) (a i) -> p c a t i", c=2, i=4),
             )
-            nc.vector.quantize_mx(out=hc[:, j, :].bitcast(FP8X4), scales=hs[:, j, :], in_=hg[:])
+            live[("hg", t)] = hg
 
-        def prep_x(i, c):
-            grp = grpp.tile([P, 4096], BF16, tag="grp", align_bytes=64)
-            regroup(
-                nc,
-                grp[:].rearrange("p (k n t) -> p k n t", k=8, t=4),
-                xraws[(i, c)][:].rearrange("p k (t n) -> p k t n", t=4),
-                V_BLOCKS,
-            )
-            xc = xp.tile([P, 1024], U32, tag="xc", align_bytes=64)
-            xs = xp.tile([P, 1024], U8, tag="xs", align_bytes=64)
-            nc.vector.quantize_mx(out=xc[:].bitcast(FP8X4), scales=xs[:], in_=grp[:])
-            return (xc, xs)
+        def h_quantise(t):
+            nc.vector.quantize_mx(out=hc[:, t, :].bitcast(FP8X4), scales=hs[:, t, :], in_=live[("hg", t)][:])
 
-        def stage2(i, xq):
-            j = i // 2
-            i2 = i % 2
-            oT = work2.tile([P, P], F32, tag="oT")
+        def stage2_mm(i):
+            banks = []
             for hh in range(2):
                 s2 = psum.tile([P, 512], F32, tag="s2")
                 for kq in range(4):
                     kk = 4 * hh + kq
                     for c in range(2):
-                        off = (c * 2 + i2) * 128
+                        xq = live[("c", 2 * i + c)]
                         nc.tensor.matmul_mx(
                             out=s2[:, kq * 128:(kq + 1) * 128],
-                            lhsT=xq[c][0][:, kk * 128:(kk + 1) * 128].bitcast(FP8X4),
-                            lhsT_scale=xq[c][1][:, kk * 128:(kk + 1) * 128],
-                            rhs=hc[:, j, off:off + 128].bitcast(FP8X4),
-                            rhs_scale=hs[:, j, off:off + 128],
+                            lhsT=xq[0][:, kk * 128:(kk + 1) * 128].bitcast(FP8X4),
+                            lhsT_scale=xq[1][:, kk * 128:(kk + 1) * 128],
+                            rhs=hc[:, i, c * 128:(c + 1) * 128].bitcast(FP8X4),
+                            rhs_scale=hs[:, i, c * 128:(c + 1) * 128],
                             start=(c == 0),
                             stop=(c == 1),
                         )
-                nc.vector.tensor_tensor(
+                banks.append(s2)
+            live[("s2", i)] = banks
+
+        def stage2_pick(i):
+            oT = work2.tile([P, P], F32, tag="oT")
+            for hh in range(2):
+                nc.scalar.copy(
                     out=oT[:].rearrange("p (b k) -> p b k", k=8)[:, :, 4 * hh:4 * hh + 4],
-                    in0=s2[:].rearrange("p (x y) -> p x y", y=16)[:, 4 * hh:4 * hh + 28:9, :].rearrange("p q b -> p b q"),
-                    in1=biasT[:, 0:NK].rearrange("p (k i) -> p i k", i=8)[:, i:i + 1, 4 * hh:4 * hh + 4].to_broadcast([P, NB, 4]),
-                    op=ALU.add,
+                    in_=live[("s2", i)][hh][:].rearrange("p (x y) -> p x y", y=16)[:, 4 * hh:4 * hh + 28:9, :].rearrange("p q b -> p b q"),
                 )
             ot = psum.tile([P, P], F32, tag="tp")
-            nc.tensor.transpose(ot[:], oT[:], ident[:])
-            nc.scalar.copy(out=o_all[:, i * 128:(i + 1) * 128], in_=ot[:])
+            nc.tensor.matmul(out=ot[:], lhsT=oT[:], rhs=ident[:], is_transpose=True, start=True, stop=False)
+            nc.tensor.matmul(out=ot[:], lhsT=bexp[:, i, :], rhs=ident[:], is_transpose=True, start=False, stop=True)
+            live[("ot", i)] = ot
+
+        def stage2_store(i):
+            nc.scalar.copy(out=o_all[:, i * 128:(i + 1) * 128], in_=live[("ot", i)][:])
             nc.scalar.dma_start(out=outv[:, i * 128:(i + 1) * 128], in_=o_all[:, i * 128:(i + 1) * 128])
 
-        prep_w2(0)
-        prep_ff(0)
-        for g in range(1, 4):
-            prep_w2(g)
-        for j in range(4):
-            if j > 0:
-                prep_ff(j)
-            zps = [stage1(2 * j), stage1(2 * j + 1)]
-            flip_h(j, zps)
-        bps = psum.tile([P, P], BF16, tag="tp")
-        nc.tensor.transpose(bps[:], braw[:], identb[:])
-        biasT = const.tile([P, P], F32)
-        nc.vector.tensor_copy(out=biasT[:], in_=bps[:])
-        for i in range(8):
-            xq = [prep_x(i, 0), prep_x(i, 1)]
-            stage2(i, xq)
+        for m in range(n_ticks):
+            key = plan[m] if m < len(plan) else None
+            prev = plan[m - 1] if 0 < m <= len(plan) else None
+            if tile_at(m, LAG["FT"]) >= 0:
+                ff_transpose(tile_at(m, LAG["FT"]))
+            for i in range(NT):
+                if o_tick[i] == m:
+                    stage2_mm(i)
+            if tile_at(m, LAG["E"]) >= 0:
+                stage1_out(tile_at(m, LAG["E"]))
+            if tile_at(m, LAG["SQ"]) >= 0:
+                variance(tile_at(m, LAG["SQ"]))
+            if key is not None:
+                regroup_s(key, V_BLOCKS, V_BLOCKS + S_FIRST)
+            for i in range(NT):
+                if o_tick[i] + LAG["OE"] == m:
+                    stage2_pick(i)
+            if tile_at(m, LAG["R"]) >= 0:
+                norm_factors(tile_at(m, LAG["R"]))
+                norm_flip(tile_at(m, LAG["R"]))
+            if key is not None:
+                regroup_v(key, V_BLOCKS)
+            if prev is not None:
+                quantise_bulk(prev)
+            if tile_at(m, LAG["MM"]) >= 0:
+                stage1_mm(tile_at(m, LAG["MM"]))
+            if tile_at(m, LAG["FE"]) >= 0:
+                ff_out(tile_at(m, LAG["FE"]))
+            if tile_at(m, LAG["T"]) >= 0:
+                residual(tile_at(m, LAG["T"]))
+            if m == CONST_TICK:
+                consts()
+            if tile_at(m, LAG["ZE"]) >= 0:
+                gain_shift(tile_at(m, LAG["ZE"]))
+            if tile_at(m, LAG["FQ"]) >= 0:
+                ff_quantise(tile_at(m, LAG["FQ"]))
+            if tile_at(m, LAG["HR"]) >= 0:
+                h_regroup(tile_at(m, LAG["HR"]))
+            if key is not None:
+                regroup_s(key, V_BLOCKS + S_FIRST, 8)
+            for i in range(NT):
+                if o_tick[i] + LAG["OC"] == m:
+                    stage2_store(i)
+            if tile_at(m, LAG["HQ"]) >= 0:
+                h_quantise(tile_at(m, LAG["HQ"]))

@@ -21,14 +21,16 @@ NT = 8
 EPS = 1e-5
 FLOPS = 2 * NB * NK * FF * D + 2 * NB * NK * D * NG
 
-V_BLOCKS = 4
-S_FIRST = 1
-LAG = {"FT": 0, "FE": 2, "FQ": 3, "T": 3, "MM": 5, "E": 7, "SQ": 8, "R": 8, "ZE": 11, "HR": 11, "HQ": 12, "O2": 14, "OE": 3, "OC": 7}
-SPARSE_UNTIL = 18
-PRE_BULK = 4
-PRE_F = 2
-PRE_T = 4
-CONST_TICK = 6
+V_BLOCKS_W = 4
+V_BLOCKS_X = 5
+LAG = {"FT": 1, "FE": 1, "FQ": 2, "T": 3, "MM": 5, "E": 6, "SQ": 8, "R": 8, "NZ": 10, "ZT": 11, "ZE": 12, "HR": 13, "HQ": 13, "O2": 15, "OQ": 0, "OE": 1, "OC": 3}
+SPARSE_UNTIL = 20
+PRE_BULK = 3
+PRE_F = 3
+PRE_T = 2
+B2_TICK = 1
+GAIN_LOAD_TICK = 2
+CONST_TICK = 11
 
 
 def bulk_plan():
@@ -56,14 +58,14 @@ def tile_mldecoder_pb_kernel(tc, ff_hid, tgt, w2, b2, g3, be3, dup_pool, dup_bia
     ffv = ff_hid.rearrange("b (kk i) f -> (b kk) i f", i=8)
     tgv = tgt.rearrange("b (kk i) d -> (b kk) i d", i=8)
     w2v = w2.rearrange("(g u q e) n -> g q u (e n)", g=4, u=2, e=2)
-    dv = dup_pool.rearrange("(kk i) (c p j) g -> i c p kk (j g)", i=8, c=2, j=4)
+    dv = dup_pool.rearrange("(hh kq i) (c p j) g -> i hh c p kq (j g)", hh=2, i=8, c=2, j=4)
     outv = out.rearrange("b (kk x) -> (b kk) x", kk=8)
     plan = bulk_plan()
     q_tick = {}
     for m in range(len(plan)):
         if plan[m] is not None:
             q_tick[plan[m]] = m + 1
-    o_tick = [max(2 * i + LAG["O2"], q_tick[("x", 2 * i + 1)] + 1) for i in range(NT)]
+    o_tick = [max(2 * (s // 2) + LAG["O2"], q_tick[("x", s)] + LAG["OQ"]) for s in range(16)]
     n_ticks = max(o_tick) + LAG["OC"] + 1
 
     with ExitStack() as ctx:
@@ -73,19 +75,17 @@ def tile_mldecoder_pb_kernel(tc, ff_hid, tgt, w2, b2, g3, be3, dup_pool, dup_bia
         frawp = ctx.enter_context(tc.tile_pool(name="frawp", bufs=3))
         grpp = ctx.enter_context(tc.tile_pool(name="grpp", bufs=3))
         xp = ctx.enter_context(tc.tile_pool(name="xp", bufs=5))
-        work1 = ctx.enter_context(tc.tile_pool(name="work1", bufs=1))
         work2 = ctx.enter_context(tc.tile_pool(name="work2", bufs=2))
-        work4 = ctx.enter_context(tc.tile_pool(name="work4", bufs=4))
+        work3 = ctx.enter_context(tc.tile_pool(name="work3", bufs=3))
         small = ctx.enter_context(tc.tile_pool(name="small", bufs=4))
         psum = ctx.enter_context(tc.psum_pool(name="psum", bufs=2))
         ctx.enter_context(tc.manual_schedule())
 
-        b2bc = const.tile([P, D], BF16)
-        nc.scalar.dma_start(out=b2bc[:], in_=b2.partition_broadcast(P))
+        brow = grpp.tile([P, 4096], BF16, tag="grp", align_bytes=64)
+        nc.vector.memset(brow[:, 0:D], 0.0)
+        nc.scalar.dma_start(out=brow[0:1, 0:D], in_=b2.rearrange("(o d) -> o d", o=1))
         g3r = const.tile([P, 2, 4], BF16)
-        nc.scalar.dma_start(out=g3r[:], in_=g3.rearrange("(c p t) -> p c t", c=2, t=4))
         be3r = const.tile([P, 2, 4], BF16)
-        nc.scalar.dma_start(out=be3r[:], in_=be3.rearrange("(c p t) -> p c t", c=2, t=4))
         braw = const.tile([P, P], BF16)
         nc.vector.memset(braw[:], 0.0)
         nc.scalar.dma_start(out=braw[0:NK, :], in_=dup_bias.rearrange("(k g) -> k g", g=NG))
@@ -108,7 +108,8 @@ def tile_mldecoder_pb_kernel(tc, ff_hid, tgt, w2, b2, g3, be3, dup_pool, dup_bia
                 raws[item[1]] = wraw[:].rearrange("p t (k n) -> p k t n", k=8)
             elif kind == "x":
                 xraw = rawp.tile([P, 8, 512], BF16, tag="raw")
-                nc.sync.dma_start(out=xraw[:], in_=dv[idx // 2, idx % 2])
+                for c in range(2):
+                    nc.sync.dma_start(out=xraw[:, 4 * c:4 * c + 4, :], in_=dv[idx // 2, idx % 2, c])
                 raws[item[1]] = xraw[:].rearrange("p k (t n) -> p k t n", t=4)
             elif kind == "f":
                 fraw = frawp.tile([P, FF], BF16, tag="fraw")
@@ -132,6 +133,9 @@ def tile_mldecoder_pb_kernel(tc, ff_hid, tgt, w2, b2, g3, be3, dup_pool, dup_bia
             out=perm[:].rearrange("p (k b) -> p k b", k=8),
             in_=ident[:].rearrange("p (b k) -> p k b", k=8),
         )
+        ones = const.tile([P, P], BF16)
+        nc.vector.memset(ones[:], 1.0)
+        b2bc = const.tile([P, D], BF16)
         g3T = const.tile([P, 8], F32)
         be3T = const.tile([P, 8], F32)
         bexp = const.tile([P, NT, P], F32)
@@ -145,6 +149,16 @@ def tile_mldecoder_pb_kernel(tc, ff_hid, tgt, w2, b2, g3, be3, dup_pool, dup_bia
         hs = keep.tile([P, NT, 256], U8, align_bytes=64)
 
         live = {}
+
+        def b2_spread():
+            for h in range(2):
+                bb = psum.tile([P, 512], F32, tag="mm")
+                nc.tensor.matmul(out=bb[:], lhsT=ones[:], rhs=brow[:, 512 * h:512 * h + 512], start=True, stop=True)
+                nc.scalar.copy(out=b2bc[:, 512 * h:512 * h + 512], in_=bb[:])
+
+        def gain_load():
+            nc.scalar.dma_start(out=g3r[:], in_=g3.rearrange("(c p t) -> p c t", c=2, t=4))
+            nc.scalar.dma_start(out=be3r[:], in_=be3.rearrange("(c p t) -> p c t", c=2, t=4))
 
         def consts():
             nc.vector.tensor_copy(out=g3T[:], in_=g3r[:].rearrange("p c t -> p (c t)"))
@@ -233,15 +247,15 @@ def tile_mldecoder_pb_kernel(tc, ff_hid, tgt, w2, b2, g3, be3, dup_pool, dup_bia
             live[("mm", t)] = banks
 
         def stage1_out(t):
-            u = work4.tile([P, D], F32, tag="u")
+            u = work3.tile([P, D], F32, tag="u")
             ssum = small.tile([P, 2], F32, tag="ssum")
             tgtb = live[("tgtb", t)]
             for h in range(2):
                 nc.vector.scalar_tensor_tensor(
-                    out=u[:, 512 * h:512 * h + 512].rearrange("p (t m) -> p m t", t=4),
-                    in0=live[("mm", t)][h][:].rearrange("p (m t) -> p m t", t=4),
+                    out=u[:, 512 * h:512 * h + 512],
+                    in0=live[("mm", t)][h][:],
                     scalar=0.0,
-                    in1=tgtb[:, 512 * h:512 * h + 512].rearrange("p (m t) -> p m t", t=4),
+                    in1=tgtb[:, 512 * h:512 * h + 512],
                     op0=ALU.add,
                     op1=ALU.add,
                     accum_out=ssum[:, h:h + 1],
@@ -255,10 +269,11 @@ def tile_mldecoder_pb_kernel(tc, ff_hid, tgt, w2, b2, g3, be3, dup_pool, dup_bia
             live[("negmean", t)] = negmean
 
         def variance(t):
-            sq = work1.tile([P, D], BF16, tag="sq")
+            zp = work2.tile([P, D], F32, tag="zp")
+            live[("zp", t)] = zp
             ssq = small.tile([P, 1], F32, tag="ssq")
             nc.scalar.activation(
-                out=sq[:], in_=live[("u", t)][:], func=ACT.Square, bias=live[("negmean", t)][:], scale=1.0,
+                out=zp[:], in_=live[("u", t)][:], func=ACT.Square, bias=live[("negmean", t)][:], scale=1.0,
                 accum_out=ssq[:],
             )
             std = small.tile([P, 1], F32, tag="std")
@@ -270,10 +285,15 @@ def tile_mldecoder_pb_kernel(tc, ff_hid, tgt, w2, b2, g3, be3, dup_pool, dup_bia
             nc.vector.reciprocal(out=rstd[:], in_=live[("std", t)][:])
             nbias = small.tile([P, 1], F32, tag="nbias")
             nc.vector.tensor_tensor(out=nbias[:], in0=live[("negmean", t)][:], in1=rstd[:], op=ALU.mult)
-            dg = work4.tile([P, P], F32, tag="dg")
-            nc.vector.tensor_scalar_mul(out=dg[:], in0=perm[:], scalar1=rstd[:, 0:1])
             live[("nbias", t)] = nbias
-            live[("dg", t)] = dg
+            live[("rstd", t)] = rstd
+
+        def normalise(t):
+            nc.scalar.activation(
+                out=live[("zp", t)][:].rearrange("p (c t m) -> p c m t", c=2, t=4),
+                in_=live[("u", t)][:].rearrange("p (c m t) -> p c m t", c=2, t=4),
+                func=ACT.Identity, bias=live[("nbias", t)][:], scale=live[("rstd", t)][:],
+            )
 
         def norm_flip(t):
             banks = []
@@ -281,14 +301,7 @@ def tile_mldecoder_pb_kernel(tc, ff_hid, tgt, w2, b2, g3, be3, dup_pool, dup_bia
                 zt = psum.tile([P, 4, P], F32, tag="zt")
                 for q in range(4):
                     pl = 4 * bk + q
-                    nc.tensor.matmul(
-                        out=zt[:, q, :], lhsT=live[("u", t)][:, pl * 128:(pl + 1) * 128], rhs=live[("dg", t)][:],
-                        start=True, stop=False,
-                    )
-                    nc.tensor.matmul(
-                        out=zt[:, q, :], lhsT=live[("nbias", t)][:, 0:1].to_broadcast([P, P]), rhs=perm[:],
-                        is_transpose=True, start=False, stop=True,
-                    )
+                    nc.tensor.transpose(zt[:, q, :], live[("zp", t)][:, pl * 128:(pl + 1) * 128], perm[:])
                 banks.append(zt)
             live[("zt", t)] = banks
 
@@ -312,35 +325,38 @@ def tile_mldecoder_pb_kernel(tc, ff_hid, tgt, w2, b2, g3, be3, dup_pool, dup_bia
         def h_quantise(t):
             nc.vector.quantize_mx(out=hc[:, t, :].bitcast(FP8X4), scales=hs[:, t, :], in_=live[("hg", t)][:])
 
-        def stage2_mm(i):
-            banks = []
-            for hh in range(2):
-                s2 = psum.tile([P, 512], F32, tag="s2")
-                for kq in range(4):
-                    kk = 4 * hh + kq
-                    for c in range(2):
-                        xq = live[("c", 2 * i + c)]
-                        nc.tensor.matmul_mx(
-                            out=s2[:, kq * 128:(kq + 1) * 128],
-                            lhsT=xq[0][:, kk * 128:(kk + 1) * 128].bitcast(FP8X4),
-                            lhsT_scale=xq[1][:, kk * 128:(kk + 1) * 128],
-                            rhs=hc[:, i, c * 128:(c + 1) * 128].bitcast(FP8X4),
-                            rhs_scale=hs[:, i, c * 128:(c + 1) * 128],
-                            start=(c == 0),
-                            stop=(c == 1),
-                        )
-                banks.append(s2)
-            live[("s2", i)] = banks
+        def stage2_mm(s):
+            i = s // 2
+            xq = live[("c", s)]
+            s2 = psum.tile([P, 512], F32, tag="s2")
+            for kq in range(4):
+                for c in range(2):
+                    blk = 4 * c + kq
+                    nc.tensor.matmul_mx(
+                        out=s2[:, kq * 128:(kq + 1) * 128],
+                        lhsT=xq[0][:, blk * 128:(blk + 1) * 128].bitcast(FP8X4),
+                        lhsT_scale=xq[1][:, blk * 128:(blk + 1) * 128],
+                        rhs=hc[:, i, c * 128:(c + 1) * 128].bitcast(FP8X4),
+                        rhs_scale=hs[:, i, c * 128:(c + 1) * 128],
+                        start=(c == 0),
+                        stop=(c == 1),
+                    )
+            live[("s2", s)] = s2
 
-        def stage2_pick(i):
-            oT = work2.tile([P, P], F32, tag="oT")
-            for hh in range(2):
-                nc.scalar.copy(
-                    out=oT[:].rearrange("p (b k) -> p b k", k=8)[:, :, 4 * hh:4 * hh + 4],
-                    in_=live[("s2", i)][hh][:].rearrange("p (x y) -> p x y", y=16)[:, 4 * hh:4 * hh + 28:9, :].rearrange("p q b -> p b q"),
-                )
+        def stage2_pick(s):
+            i = s // 2
+            hh = s % 2
+            if hh == 0:
+                oT = work2.tile([P, P], F32, tag="oT")
+                live[("oT", i)] = oT
+            nc.scalar.copy(
+                out=live[("oT", i)][:].rearrange("p (b k) -> p b k", k=8)[:, :, 4 * hh:4 * hh + 4],
+                in_=live[("s2", s)][:].rearrange("p (x y) -> p x y", y=16)[:, 4 * hh:4 * hh + 28:9, :].rearrange("p q b -> p b q"),
+            )
+
+        def stage2_flip(i):
             ot = psum.tile([P, P], F32, tag="tp")
-            nc.tensor.matmul(out=ot[:], lhsT=oT[:], rhs=ident[:], is_transpose=True, start=True, stop=False)
+            nc.tensor.matmul(out=ot[:], lhsT=live[("oT", i)][:], rhs=ident[:], is_transpose=True, start=True, stop=False)
             nc.tensor.matmul(out=ot[:], lhsT=bexp[:, i, :], rhs=ident[:], is_transpose=True, start=False, stop=True)
             live[("ot", i)] = ot
 
@@ -351,33 +367,46 @@ def tile_mldecoder_pb_kernel(tc, ff_hid, tgt, w2, b2, g3, be3, dup_pool, dup_bia
         for m in range(n_ticks):
             key = plan[m] if m < len(plan) else None
             prev = plan[m - 1] if 0 < m <= len(plan) else None
-            if tile_at(m, LAG["FT"]) >= 0:
-                ff_transpose(tile_at(m, LAG["FT"]))
-            for i in range(NT):
-                if o_tick[i] == m:
-                    stage2_mm(i)
+            nb = 0
+            if key is not None:
+                nb = V_BLOCKS_W if key[0] == "w" else V_BLOCKS_X
             if tile_at(m, LAG["E"]) >= 0:
                 stage1_out(tile_at(m, LAG["E"]))
             if tile_at(m, LAG["SQ"]) >= 0:
                 variance(tile_at(m, LAG["SQ"]))
             if key is not None:
-                regroup_s(key, V_BLOCKS, V_BLOCKS + S_FIRST)
-            for i in range(NT):
-                if o_tick[i] + LAG["OE"] == m:
-                    stage2_pick(i)
+                regroup_s(key, nb, 8)
+            for s in range(16):
+                if o_tick[s] + LAG["OE"] == m:
+                    stage2_pick(s)
             if tile_at(m, LAG["R"]) >= 0:
                 norm_factors(tile_at(m, LAG["R"]))
-                norm_flip(tile_at(m, LAG["R"]))
+            if tile_at(m, LAG["NZ"]) >= 0:
+                normalise(tile_at(m, LAG["NZ"]))
+            if tile_at(m, LAG["FT"]) >= 0:
+                ff_transpose(tile_at(m, LAG["FT"]))
+            for i in range(NT):
+                if o_tick[2 * i + 1] + LAG["OE"] == m:
+                    stage2_flip(i)
+            if tile_at(m, LAG["ZT"]) >= 0:
+                norm_flip(tile_at(m, LAG["ZT"]))
             if key is not None:
-                regroup_v(key, V_BLOCKS)
+                regroup_v(key, nb)
             if prev is not None:
                 quantise_bulk(prev)
+            for s in range(16):
+                if o_tick[s] == m:
+                    stage2_mm(s)
             if tile_at(m, LAG["MM"]) >= 0:
                 stage1_mm(tile_at(m, LAG["MM"]))
             if tile_at(m, LAG["FE"]) >= 0:
                 ff_out(tile_at(m, LAG["FE"]))
             if tile_at(m, LAG["T"]) >= 0:
                 residual(tile_at(m, LAG["T"]))
+            if m == B2_TICK:
+                b2_spread()
+            if m == GAIN_LOAD_TICK:
+                gain_load()
             if m == CONST_TICK:
                 consts()
             if tile_at(m, LAG["ZE"]) >= 0:
@@ -386,10 +415,8 @@ def tile_mldecoder_pb_kernel(tc, ff_hid, tgt, w2, b2, g3, be3, dup_pool, dup_bia
                 ff_quantise(tile_at(m, LAG["FQ"]))
             if tile_at(m, LAG["HR"]) >= 0:
                 h_regroup(tile_at(m, LAG["HR"]))
-            if key is not None:
-                regroup_s(key, V_BLOCKS + S_FIRST, 8)
             for i in range(NT):
-                if o_tick[i] + LAG["OC"] == m:
+                if o_tick[2 * i + 1] + LAG["OC"] == m:
                     stage2_store(i)
             if tile_at(m, LAG["HQ"]) >= 0:
                 h_quantise(tile_at(m, LAG["HQ"]))

@@ -7,6 +7,7 @@ F32 = mybir.dt.float32
 BF16 = mybir.dt.bfloat16
 U32 = mybir.dt.uint32
 U8 = mybir.dt.uint8
+I32 = mybir.dt.int32
 FP8X4 = mybir.dt.float8_e4m3fn_x4
 ALU = mybir.AluOpType
 ACT = mybir.ActivationFunctionType
@@ -21,16 +22,15 @@ NT = 8
 EPS = 1e-5
 FLOPS = 2 * NB * NK * FF * D + 2 * NB * NK * D * NG
 
-V_BLOCKS_W = 4
-V_BLOCKS_X = 5
-LAG = {"FT": 1, "FE": 1, "FQ": 2, "T": 3, "MM": 5, "E": 6, "SQ": 8, "R": 8, "NZ": 10, "ZT": 11, "ZE": 12, "HR": 13, "HQ": 13, "O2": 15, "OQ": 0, "OE": 1, "OC": 3}
-SPARSE_UNTIL = 20
-PRE_BULK = 3
-PRE_F = 3
-PRE_T = 2
-B2_TICK = 1
-GAIN_LOAD_TICK = 2
-CONST_TICK = 11
+V_BLOCKS = 4
+S_FIRST = 1
+LAG = {"FT": 0, "FE": 2, "FQ": 3, "T": 3, "MM": 5, "E": 7, "SQ": 8, "R": 8, "ZE": 11, "HR": 11, "HQ": 12, "O2": 14, "OE": 3, "OC": 7}
+SPARSE_UNTIL = 18
+PRE_BULK = 4
+PRE_F = 2
+PRE_T = 4
+GAIN_LOAD_AFTER = 6
+CONST_TICK = 9
 
 
 def bulk_plan():
@@ -58,14 +58,14 @@ def tile_mldecoder_pb_kernel(tc, ff_hid, tgt, w2, b2, g3, be3, dup_pool, dup_bia
     ffv = ff_hid.rearrange("b (kk i) f -> (b kk) i f", i=8)
     tgv = tgt.rearrange("b (kk i) d -> (b kk) i d", i=8)
     w2v = w2.rearrange("(g u q e) n -> g q u (e n)", g=4, u=2, e=2)
-    dv = dup_pool.rearrange("(hh kq i) (c p j) g -> i hh c p kq (j g)", hh=2, i=8, c=2, j=4)
+    dv = dup_pool.rearrange("(kk i) (c p j) g -> i c p kk (j g)", i=8, c=2, j=4)
     outv = out.rearrange("b (kk x) -> (b kk) x", kk=8)
     plan = bulk_plan()
     q_tick = {}
     for m in range(len(plan)):
         if plan[m] is not None:
             q_tick[plan[m]] = m + 1
-    o_tick = [max(2 * (s // 2) + LAG["O2"], q_tick[("x", s)] + LAG["OQ"]) for s in range(16)]
+    o_tick = [max(2 * i + LAG["O2"], q_tick[("x", 2 * i + 1)] + 1) for i in range(NT)]
     n_ticks = max(o_tick) + LAG["OC"] + 1
 
     with ExitStack() as ctx:
@@ -75,20 +75,20 @@ def tile_mldecoder_pb_kernel(tc, ff_hid, tgt, w2, b2, g3, be3, dup_pool, dup_bia
         frawp = ctx.enter_context(tc.tile_pool(name="frawp", bufs=3))
         grpp = ctx.enter_context(tc.tile_pool(name="grpp", bufs=3))
         xp = ctx.enter_context(tc.tile_pool(name="xp", bufs=5))
+        work1 = ctx.enter_context(tc.tile_pool(name="work1", bufs=1))
         work2 = ctx.enter_context(tc.tile_pool(name="work2", bufs=2))
-        work3 = ctx.enter_context(tc.tile_pool(name="work3", bufs=3))
+        work4 = ctx.enter_context(tc.tile_pool(name="work4", bufs=4))
         small = ctx.enter_context(tc.tile_pool(name="small", bufs=4))
         psum = ctx.enter_context(tc.psum_pool(name="psum", bufs=2))
-        ctx.enter_context(tc.manual_schedule())
 
         brow = grpp.tile([P, 4096], BF16, tag="grp", align_bytes=64)
-        nc.vector.memset(brow[:, 0:D], 0.0)
-        nc.scalar.dma_start(out=brow[0:1, 0:D], in_=b2.rearrange("(o d) -> o d", o=1))
+        nc.vector.memset(brow[:, 0:D].bitcast(I32), 0)
+        nc.sync.dma_start(out=brow[0:1, 0:D], in_=b2.rearrange("(o d) -> o d", o=1))
         g3r = const.tile([P, 2, 4], BF16)
         be3r = const.tile([P, 2, 4], BF16)
         braw = const.tile([P, P], BF16)
-        nc.vector.memset(braw[:], 0.0)
-        nc.scalar.dma_start(out=braw[0:NK, :], in_=dup_bias.rearrange("(k g) -> k g", g=NG))
+        nc.vector.memset(braw[:].bitcast(I32), 0)
+        nc.sync.dma_start(out=braw[0:NK, :], in_=dup_bias.rearrange("(k g) -> k g", g=NG))
 
         wanted = []
         for m in range(len(plan)):
@@ -100,6 +100,9 @@ def tile_mldecoder_pb_kernel(tc, ff_hid, tgt, w2, b2, g3, be3, dup_pool, dup_bia
                 wanted.append((2 * t + LAG["T"] - PRE_T, ("t", t // 2)))
         raws = {}
         for item in sorted(wanted, key=lambda pair: pair[0]):
+            if len(raws) == GAIN_LOAD_AFTER:
+                nc.sync.dma_start(out=g3r[:], in_=g3.rearrange("(c p t) -> p c t", c=2, t=4))
+                nc.sync.dma_start(out=be3r[:], in_=be3.rearrange("(c p t) -> p c t", c=2, t=4))
             kind = item[1][0]
             idx = item[1][1]
             if kind == "w":
@@ -108,8 +111,7 @@ def tile_mldecoder_pb_kernel(tc, ff_hid, tgt, w2, b2, g3, be3, dup_pool, dup_bia
                 raws[item[1]] = wraw[:].rearrange("p t (k n) -> p k t n", k=8)
             elif kind == "x":
                 xraw = rawp.tile([P, 8, 512], BF16, tag="raw")
-                for c in range(2):
-                    nc.sync.dma_start(out=xraw[:, 4 * c:4 * c + 4, :], in_=dv[idx // 2, idx % 2, c])
+                nc.sync.dma_start(out=xraw[:], in_=dv[idx // 2, idx % 2])
                 raws[item[1]] = xraw[:].rearrange("p k (t n) -> p k t n", t=4)
             elif kind == "f":
                 fraw = frawp.tile([P, FF], BF16, tag="fraw")
@@ -155,10 +157,6 @@ def tile_mldecoder_pb_kernel(tc, ff_hid, tgt, w2, b2, g3, be3, dup_pool, dup_bia
                 bb = psum.tile([P, 512], F32, tag="mm")
                 nc.tensor.matmul(out=bb[:], lhsT=ones[:], rhs=brow[:, 512 * h:512 * h + 512], start=True, stop=True)
                 nc.scalar.copy(out=b2bc[:, 512 * h:512 * h + 512], in_=bb[:])
-
-        def gain_load():
-            nc.scalar.dma_start(out=g3r[:], in_=g3.rearrange("(c p t) -> p c t", c=2, t=4))
-            nc.scalar.dma_start(out=be3r[:], in_=be3.rearrange("(c p t) -> p c t", c=2, t=4))
 
         def consts():
             nc.vector.tensor_copy(out=g3T[:], in_=g3r[:].rearrange("p c t -> p (c t)"))
@@ -247,15 +245,15 @@ def tile_mldecoder_pb_kernel(tc, ff_hid, tgt, w2, b2, g3, be3, dup_pool, dup_bia
             live[("mm", t)] = banks
 
         def stage1_out(t):
-            u = work3.tile([P, D], F32, tag="u")
+            u = work4.tile([P, D], F32, tag="u")
             ssum = small.tile([P, 2], F32, tag="ssum")
             tgtb = live[("tgtb", t)]
             for h in range(2):
                 nc.vector.scalar_tensor_tensor(
-                    out=u[:, 512 * h:512 * h + 512],
-                    in0=live[("mm", t)][h][:],
+                    out=u[:, 512 * h:512 * h + 512].rearrange("p (t m) -> p m t", t=4),
+                    in0=live[("mm", t)][h][:].rearrange("p (m t) -> p m t", t=4),
                     scalar=0.0,
-                    in1=tgtb[:, 512 * h:512 * h + 512],
+                    in1=tgtb[:, 512 * h:512 * h + 512].rearrange("p (m t) -> p m t", t=4),
                     op0=ALU.add,
                     op1=ALU.add,
                     accum_out=ssum[:, h:h + 1],
@@ -269,11 +267,10 @@ def tile_mldecoder_pb_kernel(tc, ff_hid, tgt, w2, b2, g3, be3, dup_pool, dup_bia
             live[("negmean", t)] = negmean
 
         def variance(t):
-            zp = work2.tile([P, D], F32, tag="zp")
-            live[("zp", t)] = zp
+            sq = work1.tile([P, D], BF16, tag="sq")
             ssq = small.tile([P, 1], F32, tag="ssq")
             nc.scalar.activation(
-                out=zp[:], in_=live[("u", t)][:], func=ACT.Square, bias=live[("negmean", t)][:], scale=1.0,
+                out=sq[:], in_=live[("u", t)][:], func=ACT.Square, bias=live[("negmean", t)][:], scale=1.0,
                 accum_out=ssq[:],
             )
             std = small.tile([P, 1], F32, tag="std")
@@ -285,15 +282,10 @@ def tile_mldecoder_pb_kernel(tc, ff_hid, tgt, w2, b2, g3, be3, dup_pool, dup_bia
             nc.vector.reciprocal(out=rstd[:], in_=live[("std", t)][:])
             nbias = small.tile([P, 1], F32, tag="nbias")
             nc.vector.tensor_tensor(out=nbias[:], in0=live[("negmean", t)][:], in1=rstd[:], op=ALU.mult)
+            dg = work4.tile([P, P], F32, tag="dg")
+            nc.vector.tensor_scalar_mul(out=dg[:], in0=perm[:], scalar1=rstd[:, 0:1])
             live[("nbias", t)] = nbias
-            live[("rstd", t)] = rstd
-
-        def normalise(t):
-            nc.scalar.activation(
-                out=live[("zp", t)][:].rearrange("p (c t m) -> p c m t", c=2, t=4),
-                in_=live[("u", t)][:].rearrange("p (c m t) -> p c m t", c=2, t=4),
-                func=ACT.Identity, bias=live[("nbias", t)][:], scale=live[("rstd", t)][:],
-            )
+            live[("dg", t)] = dg
 
         def norm_flip(t):
             banks = []
@@ -301,7 +293,14 @@ def tile_mldecoder_pb_kernel(tc, ff_hid, tgt, w2, b2, g3, be3, dup_pool, dup_bia
                 zt = psum.tile([P, 4, P], F32, tag="zt")
                 for q in range(4):
                     pl = 4 * bk + q
-                    nc.tensor.transpose(zt[:, q, :], live[("zp", t)][:, pl * 128:(pl + 1) * 128], perm[:])
+                    nc.tensor.matmul(
+                        out=zt[:, q, :], lhsT=live[("u", t)][:, pl * 128:(pl + 1) * 128], rhs=live[("dg", t)][:],
+                        start=True, stop=False,
+                    )
+                    nc.tensor.matmul(
+                        out=zt[:, q, :], lhsT=live[("nbias", t)][:, 0:1].to_broadcast([P, P]), rhs=perm[:],
+                        is_transpose=True, start=False, stop=True,
+                    )
                 banks.append(zt)
             live[("zt", t)] = banks
 
@@ -325,38 +324,35 @@ def tile_mldecoder_pb_kernel(tc, ff_hid, tgt, w2, b2, g3, be3, dup_pool, dup_bia
         def h_quantise(t):
             nc.vector.quantize_mx(out=hc[:, t, :].bitcast(FP8X4), scales=hs[:, t, :], in_=live[("hg", t)][:])
 
-        def stage2_mm(s):
-            i = s // 2
-            xq = live[("c", s)]
-            s2 = psum.tile([P, 512], F32, tag="s2")
-            for kq in range(4):
-                for c in range(2):
-                    blk = 4 * c + kq
-                    nc.tensor.matmul_mx(
-                        out=s2[:, kq * 128:(kq + 1) * 128],
-                        lhsT=xq[0][:, blk * 128:(blk + 1) * 128].bitcast(FP8X4),
-                        lhsT_scale=xq[1][:, blk * 128:(blk + 1) * 128],
-                        rhs=hc[:, i, c * 128:(c + 1) * 128].bitcast(FP8X4),
-                        rhs_scale=hs[:, i, c * 128:(c + 1) * 128],
-                        start=(c == 0),
-                        stop=(c == 1),
-                    )
-            live[("s2", s)] = s2
+        def stage2_mm(i):
+            banks = []
+            for hh in range(2):
+                s2 = psum.tile([P, 512], F32, tag="s2")
+                for kq in range(4):
+                    kk = 4 * hh + kq
+                    for c in range(2):
+                        xq = live[("c", 2 * i + c)]
+                        nc.tensor.matmul_mx(
+                            out=s2[:, kq * 128:(kq + 1) * 128],
+                            lhsT=xq[0][:, kk * 128:(kk + 1) * 128].bitcast(FP8X4),
+                            lhsT_scale=xq[1][:, kk * 128:(kk + 1) * 128],
+                            rhs=hc[:, i, c * 128:(c + 1) * 128].bitcast(FP8X4),
+                            rhs_scale=hs[:, i, c * 128:(c + 1) * 128],
+                            start=(c == 0),
+                            stop=(c == 1),
+                        )
+                banks.append(s2)
+            live[("s2", i)] = banks
 
-        def stage2_pick(s):
-            i = s // 2
-            hh = s % 2
-            if hh == 0:
-                oT = work2.tile([P, P], F32, tag="oT")
-                live[("oT", i)] = oT
-            nc.scalar.copy(
-                out=live[("oT", i)][:].rearrange("p (b k) -> p b k", k=8)[:, :, 4 * hh:4 * hh + 4],
-                in_=live[("s2", s)][:].rearrange("p (x y) -> p x y", y=16)[:, 4 * hh:4 * hh + 28:9, :].rearrange("p q b -> p b q"),
-            )
-
-        def stage2_flip(i):
+        def stage2_pick(i):
+            oT = work2.tile([P, P], F32, tag="oT")
+            for hh in range(2):
+                nc.scalar.copy(
+                    out=oT[:].rearrange("p (b k) -> p b k", k=8)[:, :, 4 * hh:4 * hh + 4],
+                    in_=live[("s2", i)][hh][:].rearrange("p (x y) -> p x y", y=16)[:, 4 * hh:4 * hh + 28:9, :].rearrange("p q b -> p b q"),
+                )
             ot = psum.tile([P, P], F32, tag="tp")
-            nc.tensor.matmul(out=ot[:], lhsT=live[("oT", i)][:], rhs=ident[:], is_transpose=True, start=True, stop=False)
+            nc.tensor.matmul(out=ot[:], lhsT=oT[:], rhs=ident[:], is_transpose=True, start=True, stop=False)
             nc.tensor.matmul(out=ot[:], lhsT=bexp[:, i, :], rhs=ident[:], is_transpose=True, start=False, stop=True)
             live[("ot", i)] = ot
 
@@ -364,49 +360,37 @@ def tile_mldecoder_pb_kernel(tc, ff_hid, tgt, w2, b2, g3, be3, dup_pool, dup_bia
             nc.scalar.copy(out=o_all[:, i * 128:(i + 1) * 128], in_=live[("ot", i)][:])
             nc.scalar.dma_start(out=outv[:, i * 128:(i + 1) * 128], in_=o_all[:, i * 128:(i + 1) * 128])
 
+        b2_spread()
         for m in range(n_ticks):
             key = plan[m] if m < len(plan) else None
             prev = plan[m - 1] if 0 < m <= len(plan) else None
-            nb = 0
-            if key is not None:
-                nb = V_BLOCKS_W if key[0] == "w" else V_BLOCKS_X
+            if tile_at(m, LAG["FT"]) >= 0:
+                ff_transpose(tile_at(m, LAG["FT"]))
+            for i in range(NT):
+                if o_tick[i] == m:
+                    stage2_mm(i)
             if tile_at(m, LAG["E"]) >= 0:
                 stage1_out(tile_at(m, LAG["E"]))
             if tile_at(m, LAG["SQ"]) >= 0:
                 variance(tile_at(m, LAG["SQ"]))
             if key is not None:
-                regroup_s(key, nb, 8)
-            for s in range(16):
-                if o_tick[s] + LAG["OE"] == m:
-                    stage2_pick(s)
+                regroup_s(key, V_BLOCKS, V_BLOCKS + S_FIRST)
+            for i in range(NT):
+                if o_tick[i] + LAG["OE"] == m:
+                    stage2_pick(i)
             if tile_at(m, LAG["R"]) >= 0:
                 norm_factors(tile_at(m, LAG["R"]))
-            if tile_at(m, LAG["NZ"]) >= 0:
-                normalise(tile_at(m, LAG["NZ"]))
-            if tile_at(m, LAG["FT"]) >= 0:
-                ff_transpose(tile_at(m, LAG["FT"]))
-            for i in range(NT):
-                if o_tick[2 * i + 1] + LAG["OE"] == m:
-                    stage2_flip(i)
-            if tile_at(m, LAG["ZT"]) >= 0:
-                norm_flip(tile_at(m, LAG["ZT"]))
+                norm_flip(tile_at(m, LAG["R"]))
             if key is not None:
-                regroup_v(key, nb)
+                regroup_v(key, V_BLOCKS)
             if prev is not None:
                 quantise_bulk(prev)
-            for s in range(16):
-                if o_tick[s] == m:
-                    stage2_mm(s)
             if tile_at(m, LAG["MM"]) >= 0:
                 stage1_mm(tile_at(m, LAG["MM"]))
             if tile_at(m, LAG["FE"]) >= 0:
                 ff_out(tile_at(m, LAG["FE"]))
             if tile_at(m, LAG["T"]) >= 0:
                 residual(tile_at(m, LAG["T"]))
-            if m == B2_TICK:
-                b2_spread()
-            if m == GAIN_LOAD_TICK:
-                gain_load()
             if m == CONST_TICK:
                 consts()
             if tile_at(m, LAG["ZE"]) >= 0:
@@ -415,8 +399,10 @@ def tile_mldecoder_pb_kernel(tc, ff_hid, tgt, w2, b2, g3, be3, dup_pool, dup_bia
                 ff_quantise(tile_at(m, LAG["FQ"]))
             if tile_at(m, LAG["HR"]) >= 0:
                 h_regroup(tile_at(m, LAG["HR"]))
+            if key is not None:
+                regroup_s(key, V_BLOCKS + S_FIRST, 8)
             for i in range(NT):
-                if o_tick[2 * i + 1] + LAG["OC"] == m:
+                if o_tick[i] + LAG["OC"] == m:
                     stage2_store(i)
             if tile_at(m, LAG["HQ"]) >= 0:
                 h_quantise(tile_at(m, LAG["HQ"]))

@@ -163,7 +163,7 @@ def tile_mldecoder_pb_kernel(tc, ff_hid, tgt, w2, b2, g3, be3, dup_pool, dup_bia
             nc.vector.tensor_copy(out=be3T[:], in_=be3r[:].rearrange("p c t -> p (c t)"))
             bps = psum.tile([P, P], BF16, tag="s2")
             nc.tensor.transpose(bps[:], braw[:], identb[:])
-            nc.vector.tensor_copy(
+            nc.scalar.copy(
                 out=bexp[:].rearrange("p i (b k) -> p i b k", k=8),
                 in_=bps[:, 0:NK].rearrange("p (k i) -> p i k", i=8).unsqueeze(2).to_broadcast([P, NT, NB, 8]),
             )
@@ -281,9 +281,9 @@ def tile_mldecoder_pb_kernel(tc, ff_hid, tgt, w2, b2, g3, be3, dup_pool, dup_bia
             rstd = small.tile([P, 1], F32, tag="rstd")
             nc.vector.reciprocal(out=rstd[:], in_=live[("std", t)][:])
             nbias = small.tile([P, 1], F32, tag="nbias")
-            nc.vector.tensor_tensor(out=nbias[:], in0=live[("negmean", t)][:], in1=rstd[:], op=ALU.mult)
+            nc.scalar.activation(out=nbias[:], in_=live[("negmean", t)][:], func=ACT.Copy, scale=rstd[:, 0:1])
             dg = work4.tile([P, P], F32, tag="dg")
-            nc.vector.tensor_scalar_mul(out=dg[:], in0=perm[:], scalar1=rstd[:, 0:1])
+            nc.scalar.activation(out=dg[:], in_=perm[:], func=ACT.Copy, scale=rstd[:, 0:1])
             live[("nbias", t)] = nbias
             live[("dg", t)] = dg
 

@@ -22,9 +22,8 @@ NT = 8
 EPS = 1e-5
 FLOPS = 2 * NB * NK * FF * D + 2 * NB * NK * D * NG
 
-V_BLOCKS = 4
 S_FIRST = 1
-LAG = {"FT": 0, "FE": 2, "FQ": 3, "T": 3, "MM": 5, "E": 7, "SQ": 8, "R": 8, "ZE": 11, "HR": 11, "HQ": 12, "O2": 14, "OE": 3, "OC": 7}
+LAG = {"FT": 0, "FE": 2, "FQ": 3, "T": 3, "MM": 5, "E": 7, "SQ": 8, "R": 8, "ZE": 11, "HR": 11, "HQ": 12, "O2": 14, "OE": 1, "OC": 2}
 SPARSE_UNTIL = 18
 PRE_BULK = 4
 PRE_F = 2
@@ -43,7 +42,7 @@ def bulk_plan():
         else:
             plan.append(("x", s))
             s += 1
-    return plan
+    return plan[:-1] + [("h", 0), ("h", 1)]
 
 
 def tile_at(m, lag):
@@ -65,8 +64,9 @@ def tile_mldecoder_pb_kernel(tc, ff_hid, tgt, w2, b2, g3, be3, dup_pool, dup_bia
     for m in range(len(plan)):
         if plan[m] is not None:
             q_tick[plan[m]] = m + 1
-    o_tick = [max(2 * i + LAG["O2"], q_tick[("x", 2 * i + 1)] + 1) for i in range(NT)]
-    n_ticks = max(o_tick) + LAG["OC"] + 1
+    o_tick = [max(2 * i + LAG["O2"], q_tick[("x", 2 * i + 1)] + 1) for i in range(NT - 1)]
+    last_tick = [q_tick[("x", 14)] + 1, q_tick[("h", 0)] + 1, q_tick[("h", 1)] + 1]
+    n_ticks = max(max(o_tick) + LAG["OC"], last_tick[2]) + 1
 
     with ExitStack() as ctx:
         const = ctx.enter_context(tc.tile_pool(name="const", bufs=1))
@@ -92,8 +92,8 @@ def tile_mldecoder_pb_kernel(tc, ff_hid, tgt, w2, b2, g3, be3, dup_pool, dup_bia
 
         wanted = []
         for m in range(len(plan)):
-            if plan[m] is not None:
-                wanted.append((m - PRE_BULK, plan[m]))
+            if plan[m] is not None and plan[m] != ("h", 1):
+                wanted.append((m - PRE_BULK, ("x", 15) if plan[m] == ("h", 0) else plan[m]))
         for t in range(NT):
             wanted.append((2 * t + LAG["FT"] - PRE_F, ("f", t)))
             if t % 2 == 0:
@@ -174,19 +174,24 @@ def tile_mldecoder_pb_kernel(tc, ff_hid, tgt, w2, b2, g3, be3, dup_pool, dup_bia
                 live[("g", key)] = grp
             return live[("g", key)]
 
+        def src_of(key):
+            if key[0] == "h":
+                return raws[("x", 15)][:, 4 * key[1]:4 * key[1] + 4]
+            return raws[key]
+
         def regroup_s(key, lo, hi):
             dst4 = grp_of(key)[:].rearrange("p (k n t) -> p k n t", k=8, t=4)
             for k in range(lo, hi):
                 nc.scalar.copy(
                     out=dst4[:, k].rearrange("p (c i) t -> p c t i", i=4),
-                    in_=raws[key][:, k].rearrange("p t (c i) -> p c t i", i=4),
+                    in_=src_of(key)[:, k].rearrange("p t (c i) -> p c t i", i=4),
                 )
 
         def regroup_v(key, nb):
             dst4 = grp_of(key)[:].rearrange("p (k n t) -> p k n t", k=8, t=4)
             nc.vector.tensor_copy(
                 out=dst4[:, 0:nb].rearrange("p k (c i) t -> p k c t i", i=4),
-                in_=raws[key][:, 0:nb].rearrange("p k t (c i) -> p k c t i", i=4),
+                in_=src_of(key)[:, 0:nb].rearrange("p k t (c i) -> p k c t i", i=4),
             )
 
         def quantise_bulk(key):
@@ -194,6 +199,15 @@ def tile_mldecoder_pb_kernel(tc, ff_hid, tgt, w2, b2, g3, be3, dup_pool, dup_bia
             if key[0] == "w":
                 g = key[1]
                 nc.vector.quantize_mx(out=w2c[:, g, :].bitcast(FP8X4), scales=w2s[:, g, :], in_=grp[:])
+            elif key[0] == "h":
+                if key[1] == 0:
+                    xc = xp.tile([P, 1024], U32, tag="xc", align_bytes=64)
+                    xs = xp.tile([P, 1024], U8, tag="xs", align_bytes=64)
+                    live[("c", 15)] = (xc, xs)
+                half = slice(512 * key[1], 512 * key[1] + 512)
+                nc.vector.quantize_mx(
+                    out=live[("c", 15)][0][:, half].bitcast(FP8X4), scales=live[("c", 15)][1][:, half], in_=grp[:, 0:2048],
+                )
             else:
                 xc = xp.tile([P, 1024], U32, tag="xc", align_bytes=64)
                 xs = xp.tile([P, 1024], U8, tag="xs", align_bytes=64)
@@ -356,6 +370,35 @@ def tile_mldecoder_pb_kernel(tc, ff_hid, tgt, w2, b2, g3, be3, dup_pool, dup_bia
             nc.tensor.matmul(out=ot[:], lhsT=bexp[:, i, :], rhs=ident[:], is_transpose=True, start=False, stop=True)
             live[("ot", i)] = ot
 
+        def last_mm(c, hh):
+            xq = live[("c", 14 + c)]
+            s2 = psum.tile([P, 512], F32, tag="s2")
+            for kq in range(4):
+                kk = 4 * hh + kq
+                nc.tensor.matmul_mx(
+                    out=s2[:, kq * 128:(kq + 1) * 128],
+                    lhsT=xq[0][:, kk * 128:(kk + 1) * 128].bitcast(FP8X4),
+                    lhsT_scale=xq[1][:, kk * 128:(kk + 1) * 128],
+                    rhs=hc[:, NT - 1, c * 128:(c + 1) * 128].bitcast(FP8X4),
+                    rhs_scale=hs[:, NT - 1, c * 128:(c + 1) * 128],
+                    start=True,
+                    stop=True,
+                )
+            if hh == 0:
+                oT = work2.tile([P, P], F32, tag="oT")
+                live[("oT", c)] = oT
+            nc.scalar.copy(
+                out=live[("oT", c)][:].rearrange("p (b k) -> p b k", k=8)[:, :, 4 * hh:4 * hh + 4],
+                in_=s2[:].rearrange("p (x y) -> p x y", y=16)[:, 4 * hh:4 * hh + 28:9, :].rearrange("p q b -> p b q"),
+            )
+
+        def last_flip():
+            ot = psum.tile([P, P], F32, tag="tp")
+            nc.tensor.matmul(out=ot[:], lhsT=bexp[:, NT - 1, :], rhs=ident[:], is_transpose=True, start=True, stop=False)
+            nc.tensor.matmul(out=ot[:], lhsT=live[("oT", 0)][:], rhs=ident[:], is_transpose=True, start=False, stop=False)
+            nc.tensor.matmul(out=ot[:], lhsT=live[("oT", 1)][:], rhs=ident[:], is_transpose=True, start=False, stop=True)
+            live[("ot", NT - 1)] = ot
+
         def stage2_store(i):
             nc.scalar.copy(out=o_all[:, i * 128:(i + 1) * 128], in_=live[("ot", i)][:])
             nc.scalar.dma_start(out=outv[:, i * 128:(i + 1) * 128], in_=o_all[:, i * 128:(i + 1) * 128])
@@ -366,23 +409,36 @@ def tile_mldecoder_pb_kernel(tc, ff_hid, tgt, w2, b2, g3, be3, dup_pool, dup_bia
             prev = plan[m - 1] if 0 < m <= len(plan) else None
             if tile_at(m, LAG["FT"]) >= 0:
                 ff_transpose(tile_at(m, LAG["FT"]))
-            for i in range(NT):
+            for i in range(NT - 1):
                 if o_tick[i] == m:
                     stage2_mm(i)
             if tile_at(m, LAG["E"]) >= 0:
                 stage1_out(tile_at(m, LAG["E"]))
             if tile_at(m, LAG["SQ"]) >= 0:
                 variance(tile_at(m, LAG["SQ"]))
+            blocks = 8
+            if key is not None and key[0] == "h":
+                blocks = 4
+            nb = blocks // 2
             if key is not None:
-                regroup_s(key, V_BLOCKS, V_BLOCKS + S_FIRST)
-            for i in range(NT):
+                regroup_s(key, nb, nb + S_FIRST)
+            for i in range(NT - 1):
                 if o_tick[i] + LAG["OE"] == m:
                     stage2_pick(i)
+            if m == last_tick[0]:
+                last_mm(0, 0)
+                last_mm(0, 1)
+            if m == last_tick[1]:
+                last_mm(1, 0)
+            if m == last_tick[2]:
+                last_mm(1, 1)
+                last_flip()
+                stage2_store(NT - 1)
             if tile_at(m, LAG["R"]) >= 0:
                 norm_factors(tile_at(m, LAG["R"]))
                 norm_flip(tile_at(m, LAG["R"]))
             if key is not None:
-                regroup_v(key, V_BLOCKS)
+                regroup_v(key, nb)
             if prev is not None:
                 quantise_bulk(prev)
             if tile_at(m, LAG["MM"]) >= 0:
@@ -400,8 +456,8 @@ def tile_mldecoder_pb_kernel(tc, ff_hid, tgt, w2, b2, g3, be3, dup_pool, dup_bia
             if tile_at(m, LAG["HR"]) >= 0:
                 h_regroup(tile_at(m, LAG["HR"]))
             if key is not None:
-                regroup_s(key, V_BLOCKS + S_FIRST, 8)
-            for i in range(NT):
+                regroup_s(key, nb + S_FIRST, blocks)
+            for i in range(NT - 1):
                 if o_tick[i] + LAG["OC"] == m:
                     stage2_store(i)
             if tile_at(m, LAG["HQ"]) >= 0:

@@ -22,14 +22,16 @@ NT = 8
 EPS = 1e-5
 FLOPS = 2 * NB * NK * FF * D + 2 * NB * NK * D * NG
 
+V_BLOCKS = 4
 S_FIRST = 1
-LAG = {"FT": 0, "FE": 2, "FQ": 3, "T": 3, "MM": 5, "E": 7, "SQ": 8, "R": 8, "ZE": 11, "HR": 11, "HQ": 12, "O2": 14, "OE": 1, "OC": 2}
+LAG = {"FT": 0, "FE": 2, "FQ": 3, "T": 3, "MM": 5, "E": 7, "SQ": 8, "R": 8, "ZE": 11, "HR": 11, "HQ": 12, "O2": 14, "OE": 3, "OC": 7}
 SPARSE_UNTIL = 18
 PRE_BULK = 4
 PRE_F = 2
 PRE_T = 4
 GAIN_LOAD_AFTER = 6
 CONST_TICK = 9
+SCALAR_NORM_FROM = 5
 
 
 def bulk_plan():
@@ -42,7 +44,7 @@ def bulk_plan():
         else:
             plan.append(("x", s))
             s += 1
-    return plan[:-1] + [("h", 0), ("h", 1)]
+    return plan
 
 
 def tile_at(m, lag):
@@ -64,9 +66,8 @@ def tile_mldecoder_pb_kernel(tc, ff_hid, tgt, w2, b2, g3, be3, dup_pool, dup_bia
     for m in range(len(plan)):
         if plan[m] is not None:
             q_tick[plan[m]] = m + 1
-    o_tick = [max(2 * i + LAG["O2"], q_tick[("x", 2 * i + 1)] + 1) for i in range(NT - 1)]
-    last_tick = [q_tick[("x", 14)] + 1, q_tick[("h", 0)] + 1, q_tick[("h", 1)] + 1]
-    n_ticks = max(max(o_tick) + LAG["OC"], last_tick[2]) + 1
+    o_tick = [max(2 * i + LAG["O2"], q_tick[("x", 2 * i + 1)] + 1) for i in range(NT)]
+    n_ticks = max(o_tick) + LAG["OC"] + 1
 
     with ExitStack() as ctx:
         const = ctx.enter_context(tc.tile_pool(name="const", bufs=1))
@@ -92,8 +93,8 @@ def tile_mldecoder_pb_kernel(tc, ff_hid, tgt, w2, b2, g3, be3, dup_pool, dup_bia
 
         wanted = []
         for m in range(len(plan)):
-            if plan[m] is not None and plan[m] != ("h", 1):
-                wanted.append((m - PRE_BULK, ("x", 15) if plan[m] == ("h", 0) else plan[m]))
+            if plan[m] is not None:
+                wanted.append((m - PRE_BULK, plan[m]))
         for t in range(NT):
             wanted.append((2 * t + LAG["FT"] - PRE_F, ("f", t)))
             if t % 2 == 0:
@@ -174,24 +175,19 @@ def tile_mldecoder_pb_kernel(tc, ff_hid, tgt, w2, b2, g3, be3, dup_pool, dup_bia
                 live[("g", key)] = grp
             return live[("g", key)]
 
-        def src_of(key):
-            if key[0] == "h":
-                return raws[("x", 15)][:, 4 * key[1]:4 * key[1] + 4]
-            return raws[key]
-
         def regroup_s(key, lo, hi):
             dst4 = grp_of(key)[:].rearrange("p (k n t) -> p k n t", k=8, t=4)
             for k in range(lo, hi):
                 nc.scalar.copy(
                     out=dst4[:, k].rearrange("p (c i) t -> p c t i", i=4),
-                    in_=src_of(key)[:, k].rearrange("p t (c i) -> p c t i", i=4),
+                    in_=raws[key][:, k].rearrange("p t (c i) -> p c t i", i=4),
                 )
 
         def regroup_v(key, nb):
             dst4 = grp_of(key)[:].rearrange("p (k n t) -> p k n t", k=8, t=4)
             nc.vector.tensor_copy(
                 out=dst4[:, 0:nb].rearrange("p k (c i) t -> p k c t i", i=4),
-                in_=src_of(key)[:, 0:nb].rearrange("p k t (c i) -> p k c t i", i=4),
+                in_=raws[key][:, 0:nb].rearrange("p k t (c i) -> p k c t i", i=4),
             )
 
         def quantise_bulk(key):
@@ -199,15 +195,6 @@ def tile_mldecoder_pb_kernel(tc, ff_hid, tgt, w2, b2, g3, be3, dup_pool, dup_bia
             if key[0] == "w":
                 g = key[1]
                 nc.vector.quantize_mx(out=w2c[:, g, :].bitcast(FP8X4), scales=w2s[:, g, :], in_=grp[:])
-            elif key[0] == "h":
-                if key[1] == 0:
-                    xc = xp.tile([P, 1024], U32, tag="xc", align_bytes=64)
-                    xs = xp.tile([P, 1024], U8, tag="xs", align_bytes=64)
-                    live[("c", 15)] = (xc, xs)
-                half = slice(512 * key[1], 512 * key[1] + 512)
-                nc.vector.quantize_mx(
-                    out=live[("c", 15)][0][:, half].bitcast(FP8X4), scales=live[("c", 15)][1][:, half], in_=grp[:, 0:2048],
-                )
             else:
                 xc = xp.tile([P, 1024], U32, tag="xc", align_bytes=64)
                 xs = xp.tile([P, 1024], U8, tag="xs", align_bytes=64)
@@ -263,8 +250,13 @@ def tile_mldecoder_pb_kernel(tc, ff_hid, tgt, w2, b2, g3, be3, dup_pool, dup_bia
             ssum = small.tile([P, 2], F32, tag="ssum")
             tgtb = live[("tgtb", t)]
             for h in range(2):
+                u_half = u[:, 512 * h:512 * h + 512]
+                if t < SCALAR_NORM_FROM:
+                    u_half = u_half.rearrange("p (t m) -> p m t", t=4)
+                else:
+                    u_half = u_half.rearrange("p (m t) -> p m t", t=4)
                 nc.vector.scalar_tensor_tensor(
-                    out=u[:, 512 * h:512 * h + 512].rearrange("p (t m) -> p m t", t=4),
+                    out=u_half,
                     in0=live[("mm", t)][h][:].rearrange("p (m t) -> p m t", t=4),
                     scalar=0.0,
                     in1=tgtb[:, 512 * h:512 * h + 512].rearrange("p (m t) -> p m t", t=4),
@@ -296,10 +288,19 @@ def tile_mldecoder_pb_kernel(tc, ff_hid, tgt, w2, b2, g3, be3, dup_pool, dup_bia
             nc.vector.reciprocal(out=rstd[:], in_=live[("std", t)][:])
             nbias = small.tile([P, 1], F32, tag="nbias")
             nc.scalar.activation(out=nbias[:], in_=live[("negmean", t)][:], func=ACT.Copy, scale=rstd[:, 0:1])
-            dg = work4.tile([P, P], F32, tag="dg")
-            nc.scalar.activation(out=dg[:], in_=perm[:], func=ACT.Copy, scale=rstd[:, 0:1])
             live[("nbias", t)] = nbias
-            live[("dg", t)] = dg
+            if t < SCALAR_NORM_FROM:
+                dg = work4.tile([P, P], F32, tag="dg")
+                nc.scalar.activation(out=dg[:], in_=perm[:], func=ACT.Copy, scale=rstd[:, 0:1])
+                live[("dg", t)] = dg
+            else:
+                zp = work2.tile([P, D], F32, tag="zp")
+                nc.scalar.activation(
+                    out=zp[:].rearrange("p (c t m) -> p c m t", c=2, t=4),
+                    in_=live[("u", t)][:].rearrange("p (c m t) -> p c m t", c=2, t=4),
+                    func=ACT.Identity, bias=nbias[:], scale=rstd[:, 0:1],
+                )
+                live[("zp", t)] = zp
 
         def norm_flip(t):
             banks = []
@@ -307,14 +308,17 @@ def tile_mldecoder_pb_kernel(tc, ff_hid, tgt, w2, b2, g3, be3, dup_pool, dup_bia
                 zt = psum.tile([P, 4, P], F32, tag="zt")
                 for q in range(4):
                     pl = 4 * bk + q
-                    nc.tensor.matmul(
-                        out=zt[:, q, :], lhsT=live[("u", t)][:, pl * 128:(pl + 1) * 128], rhs=live[("dg", t)][:],
-                        start=True, stop=False,
-                    )
-                    nc.tensor.matmul(
-                        out=zt[:, q, :], lhsT=live[("nbias", t)][:, 0:1].to_broadcast([P, P]), rhs=perm[:],
-                        is_transpose=True, start=False, stop=True,
-                    )
+                    if t < SCALAR_NORM_FROM:
+                        nc.tensor.matmul(
+                            out=zt[:, q, :], lhsT=live[("u", t)][:, pl * 128:(pl + 1) * 128], rhs=live[("dg", t)][:],
+                            start=True, stop=False,
+                        )
+                        nc.tensor.matmul(
+                            out=zt[:, q, :], lhsT=live[("nbias", t)][:, 0:1].to_broadcast([P, P]), rhs=perm[:],
+                            is_transpose=True, start=False, stop=True,
+                        )
+                    else:
+                        nc.tensor.transpose(zt[:, q, :], live[("zp", t)][:, pl * 128:(pl + 1) * 128], perm[:])
                 banks.append(zt)
             live[("zt", t)] = banks
 
@@ -370,35 +374,6 @@ def tile_mldecoder_pb_kernel(tc, ff_hid, tgt, w2, b2, g3, be3, dup_pool, dup_bia
             nc.tensor.matmul(out=ot[:], lhsT=bexp[:, i, :], rhs=ident[:], is_transpose=True, start=False, stop=True)
             live[("ot", i)] = ot
 
-        def last_mm(c, hh):
-            xq = live[("c", 14 + c)]
-            s2 = psum.tile([P, 512], F32, tag="s2")
-            for kq in range(4):
-                kk = 4 * hh + kq
-                nc.tensor.matmul_mx(
-                    out=s2[:, kq * 128:(kq + 1) * 128],
-                    lhsT=xq[0][:, kk * 128:(kk + 1) * 128].bitcast(FP8X4),
-                    lhsT_scale=xq[1][:, kk * 128:(kk + 1) * 128],
-                    rhs=hc[:, NT - 1, c * 128:(c + 1) * 128].bitcast(FP8X4),
-                    rhs_scale=hs[:, NT - 1, c * 128:(c + 1) * 128],
-                    start=True,
-                    stop=True,
-                )
-            if hh == 0:
-                oT = work2.tile([P, P], F32, tag="oT")
-                live[("oT", c)] = oT
-            nc.scalar.copy(
-                out=live[("oT", c)][:].rearrange("p (b k) -> p b k", k=8)[:, :, 4 * hh:4 * hh + 4],
-                in_=s2[:].rearrange("p (x y) -> p x y", y=16)[:, 4 * hh:4 * hh + 28:9, :].rearrange("p q b -> p b q"),
-            )
-
-        def last_flip():
-            ot = psum.tile([P, P], F32, tag="tp")
-            nc.tensor.matmul(out=ot[:], lhsT=bexp[:, NT - 1, :], rhs=ident[:], is_transpose=True, start=True, stop=False)
-            nc.tensor.matmul(out=ot[:], lhsT=live[("oT", 0)][:], rhs=ident[:], is_transpose=True, start=False, stop=False)
-            nc.tensor.matmul(out=ot[:], lhsT=live[("oT", 1)][:], rhs=ident[:], is_transpose=True, start=False, stop=True)
-            live[("ot", NT - 1)] = ot
-
         def stage2_store(i):
             nc.scalar.copy(out=o_all[:, i * 128:(i + 1) * 128], in_=live[("ot", i)][:])
             nc.scalar.dma_start(out=outv[:, i * 128:(i + 1) * 128], in_=o_all[:, i * 128:(i + 1) * 128])
@@ -409,36 +384,23 @@ def tile_mldecoder_pb_kernel(tc, ff_hid, tgt, w2, b2, g3, be3, dup_pool, dup_bia
             prev = plan[m - 1] if 0 < m <= len(plan) else None
             if tile_at(m, LAG["FT"]) >= 0:
                 ff_transpose(tile_at(m, LAG["FT"]))
-            for i in range(NT - 1):
+            for i in range(NT):
                 if o_tick[i] == m:
                     stage2_mm(i)
             if tile_at(m, LAG["E"]) >= 0:
                 stage1_out(tile_at(m, LAG["E"]))
             if tile_at(m, LAG["SQ"]) >= 0:
                 variance(tile_at(m, LAG["SQ"]))
-            blocks = 8
-            if key is not None and key[0] == "h":
-                blocks = 4
-            nb = blocks // 2
             if key is not None:
-                regroup_s(key, nb, nb + S_FIRST)
-            for i in range(NT - 1):
+                regroup_s(key, V_BLOCKS, V_BLOCKS + S_FIRST)
+            for i in range(NT):
                 if o_tick[i] + LAG["OE"] == m:
                     stage2_pick(i)
-            if m == last_tick[0]:
-                last_mm(0, 0)
-                last_mm(0, 1)
-            if m == last_tick[1]:
-                last_mm(1, 0)
-            if m == last_tick[2]:
-                last_mm(1, 1)
-                last_flip()
-                stage2_store(NT - 1)
             if tile_at(m, LAG["R"]) >= 0:
                 norm_factors(tile_at(m, LAG["R"]))
                 norm_flip(tile_at(m, LAG["R"]))
             if key is not None:
-                regroup_v(key, nb)
+                regroup_v(key, V_BLOCKS)
             if prev is not None:
                 quantise_bulk(prev)
             if tile_at(m, LAG["MM"]) >= 0:
@@ -456,8 +418,8 @@ def tile_mldecoder_pb_kernel(tc, ff_hid, tgt, w2, b2, g3, be3, dup_pool, dup_bia
             if tile_at(m, LAG["HR"]) >= 0:
                 h_regroup(tile_at(m, LAG["HR"]))
             if key is not None:
-                regroup_s(key, nb + S_FIRST, blocks)
-            for i in range(NT - 1):
+                regroup_s(key, V_BLOCKS + S_FIRST, 8)
+            for i in range(NT):
                 if o_tick[i] + LAG["OC"] == m:
                     stage2_store(i)
             if tile_at(m, LAG["HQ"]) >= 0:

from contextlib import ExitStack

import concourse.mybir as mybir
from concourse.masks import make_identity

F32 = mybir.dt.float32
BF16 = mybir.dt.bfloat16
U32 = mybir.dt.uint32
U8 = mybir.dt.uint8
I32 = mybir.dt.int32
FP8X4 = mybir.dt.float8_e4m3fn_x4
ALU = mybir.AluOpType
ACT = mybir.ActivationFunctionType

P = 128
NB = 16
NK = 64
NG = 128
D = 1024
FF = 2048
NT = 8
EPS = 1e-5
FLOPS = 2 * NB * NK * FF * D + 2 * NB * NK * D * NG

V_BLOCKS = 4
S_FIRST = 1
LAG = {"FT": 0, "FE": 2, "FQ": 3, "T": 3, "MM": 5, "E": 7, "SQ": 8, "R": 8, "ZE": 11, "HR": 11, "HQ": 12, "O2": 14, "OE": 3, "OC": 7}
SPARSE_UNTIL = 18
PRE_BULK = 4
PRE_F = 2
PRE_T = 4
GAIN_LOAD_AFTER = 6
CONST_TICK = 9
SCALAR_NORM_FROM = 5


def bulk_plan():
    plan = [("w", g) for g in range(4)]
    s = 0
    while s < 16:
        m = len(plan)
        if m < SPARSE_UNTIL and m % 2 == 0:
            plan.append(None)
        else:
            plan.append(("x", s))
            s += 1
    return plan


def tile_at(m, lag):
    t = m - lag
    if t >= 0 and t % 2 == 0 and t // 2 < NT:
        return t // 2
    return -1


def tile_mldecoder_pb_kernel(tc, ff_hid, tgt, w2, b2, g3, be3, dup_pool, dup_bias, out):
    nc = tc.nc
    ffv = ff_hid.rearrange("b (kk i) f -> (b kk) i f", i=8)
    tgv = tgt.rearrange("b (kk i) d -> (b kk) i d", i=8)
    w2v = w2.rearrange("(g u q e) n -> g q u (e n)", g=4, u=2, e=2)
    dv = dup_pool.rearrange("(kk i) (c p j) g -> i c p kk (j g)", i=8, c=2, j=4)
    outv = out.rearrange("b (kk x) -> (b kk) x", kk=8)
    plan = bulk_plan()
    q_tick = {}
    for m in range(len(plan)):
        if plan[m] is not None:
            q_tick[plan[m]] = m + 1
    o_tick = [max(2 * i + LAG["O2"], q_tick[("x", 2 * i + 1)] + 1) for i in range(NT)]
    n_ticks = max(o_tick) + LAG["OC"] + 1

    with ExitStack() as ctx:
        const = ctx.enter_context(tc.tile_pool(name="const", bufs=1))
        keep = ctx.enter_context(tc.tile_pool(name="keep", bufs=1))
        rawp = ctx.enter_context(tc.tile_pool(name="rawp", bufs=6))
        frawp = ctx.enter_context(tc.tile_pool(name="frawp", bufs=3))
        grpp = ctx.enter_context(tc.tile_pool(name="grpp", bufs=3))
        xp = ctx.enter_context(tc.tile_pool(name="xp", bufs=5))
        work1 = ctx.enter_context(tc.tile_pool(name="work1", bufs=1))
        work2 = ctx.enter_context(tc.tile_pool(name="work2", bufs=2))
        work4 = ctx.enter_context(tc.tile_pool(name="work4", bufs=4))
        small = ctx.enter_context(tc.tile_pool(name="small", bufs=4))
        psum = ctx.enter_context(tc.psum_pool(name="psum", bufs=2))

        brow = grpp.tile([P, 4096], BF16, tag="grp", align_bytes=64)
        nc.vector.memset(brow[:, 0:D].bitcast(I32), 0)
        nc.sync.dma_start(out=brow[0:1, 0:D], in_=b2.rearrange("(o d) -> o d", o=1))
        g3r = const.tile([P, 2, 4], BF16)
        be3r = const.tile([P, 2, 4], BF16)
        braw = const.tile([P, P], BF16)
        nc.vector.memset(braw[:].bitcast(I32), 0)
        nc.sync.dma_start(out=braw[0:NK, :], in_=dup_bias.rearrange("(k g) -> k g", g=NG))

        wanted = []
        for m in range(len(plan)):
            if plan[m] is not None:
                wanted.append((m - PRE_BULK, plan[m]))
        for t in range(NT):
            wanted.append((2 * t + LAG["FT"] - PRE_F, ("f", t)))
            if t % 2 == 0:
                wanted.append((2 * t + LAG["T"] - PRE_T, ("t", t // 2)))
        raws = {}
        for item in sorted(wanted, key=lambda pair: pair[0]):
            if len(raws) == GAIN_LOAD_AFTER:
                nc.sync.dma_start(out=g3r[:], in_=g3.rearrange("(c p t) -> p c t", c=2, t=4))
                nc.sync.dma_start(out=be3r[:], in_=be3.rearrange("(c p t) -> p c t", c=2, t=4))
            kind = item[1][0]
            idx = item[1][1]
            if kind == "w":
                wraw = rawp.tile([P, 4, D], BF16, tag="raw")
                nc.sync.dma_start(out=wraw[:].rearrange("p (u e) n -> p u (e n)", u=2), in_=w2v[idx])
                raws[item[1]] = wraw[:].rearrange("p t (k n) -> p k t n", k=8)
            elif kind == "x":
                xraw = rawp.tile([P, 8, 512], BF16, tag="raw")
                nc.sync.dma_start(out=xraw[:], in_=dv[idx // 2, idx % 2])
                raws[item[1]] = xraw[:].rearrange("p k (t n) -> p k t n", t=4)
            elif kind == "f":
                fraw = frawp.tile([P, FF], BF16, tag="fraw")
                nc.sync.dma_start(out=fraw[:], in_=ffv[:, idx, :])
                raws[item[1]] = fraw
            else:
                traw = work2.tile([P, 2, D], BF16, tag="traw")
                nc.sync.dma_start(out=traw[:], in_=tgv[:, 2 * idx:2 * idx + 2, :])
                raws[item[1]] = traw

        eps = const.tile([P, 1], F32)
        nc.vector.memset(eps[:], EPS)
        warm = const.tile([P, 1], F32)
        nc.scalar.activation(out=warm[:], in_=eps[:], func=ACT.Sqrt)
        ident = const.tile([P, P], F32)
        make_identity(nc, ident[:])
        identb = const.tile([P, P], BF16)
        make_identity(nc, identb[:])
        perm = const.tile([P, P], F32)
        nc.vector.tensor_copy(
            out=perm[:].rearrange("p (k b) -> p k b", k=8),
            in_=ident[:].rearrange("p (b k) -> p k b", k=8),
        )
        ones = const.tile([P, P], BF16)
        nc.vector.memset(ones[:], 1.0)
        b2bc = const.tile([P, D], BF16)
        g3T = const.tile([P, 8], F32)
        be3T = const.tile([P, 8], F32)
        bexp = const.tile([P, NT, P], F32)
        o_all = const.tile([P, D], F32)

        w2c = keep.tile([P, 4, D], U32, align_bytes=64)
        w2s = keep.tile([P, 4, D], U8, align_bytes=64)
        fc = keep.tile([P, NT, 512], U32, align_bytes=64)
        fs = keep.tile([P, NT, 512], U8, align_bytes=64)
        hc = keep.tile([P, NT, 256], U32, align_bytes=64)
        hs = keep.tile([P, NT, 256], U8, align_bytes=64)

        live = {}

        def b2_spread():
            for h in range(2):
                bb = psum.tile([P, 512], F32, tag="mm")
                nc.tensor.matmul(out=bb[:], lhsT=ones[:], rhs=brow[:, 512 * h:512 * h + 512], start=True, stop=True)
                nc.scalar.copy(out=b2bc[:, 512 * h:512 * h + 512], in_=bb[:])

        def consts():
            nc.vector.tensor_copy(out=g3T[:], in_=g3r[:].rearrange("p c t -> p (c t)"))
            nc.vector.tensor_copy(out=be3T[:], in_=be3r[:].rearrange("p c t -> p (c t)"))
            bps = psum.tile([P, P], BF16, tag="s2")
            nc.tensor.transpose(bps[:], braw[:], identb[:])
            nc.scalar.copy(
                out=bexp[:].rearrange("p i (b k) -> p i b k", k=8),
                in_=bps[:, 0:NK].rearrange("p (k i) -> p i k", i=8).unsqueeze(2).to_broadcast([P, NT, NB, 8]),
            )

        def grp_of(key):
            if ("g", key) not in live:
                grp = grpp.tile([P, 4096], BF16, tag="grp", align_bytes=64)
                live[("g", key)] = grp
            return live[("g", key)]

        def regroup_s(key, lo, hi):
            dst4 = grp_of(key)[:].rearrange("p (k n t) -> p k n t", k=8, t=4)
            for k in range(lo, hi):
                nc.scalar.copy(
                    out=dst4[:, k].rearrange("p (c i) t -> p c t i", i=4),
                    in_=raws[key][:, k].rearrange("p t (c i) -> p c t i", i=4),
                )

        def regroup_v(key, nb):
            dst4 = grp_of(key)[:].rearrange("p (k n t) -> p k n t", k=8, t=4)
            nc.vector.tensor_copy(
                out=dst4[:, 0:nb].rearrange("p k (c i) t -> p k c t i", i=4),
                in_=raws[key][:, 0:nb].rearrange("p k t (c i) -> p k c t i", i=4),
            )

        def quantise_bulk(key):
            grp = grp_of(key)
            if key[0] == "w":
                g = key[1]
                nc.vector.quantize_mx(out=w2c[:, g, :].bitcast(FP8X4), scales=w2s[:, g, :], in_=grp[:])
            else:
                xc = xp.tile([P, 1024], U32, tag="xc", align_bytes=64)
                xs = xp.tile([P, 1024], U8, tag="xs", align_bytes=64)
                nc.vector.quantize_mx(out=xc[:].bitcast(FP8X4), scales=xs[:], in_=grp[:])
                live[("c", key[1])] = (xc, xs)

        def ff_transpose(t):
            words = raws[("f", t)][:].bitcast(F32)
            banks = []
            for gp in range(2):
                tp = psum.tile([P, 2, 2, P], F32, tag="tp")
                for gq in range(2):
                    for u in range(2):
                        col = 256 * (2 * gp + gq) + 128 * u
                        nc.tensor.transpose(tp[:, gq, u, :], words[:, col:col + 128], ident[:])
                banks.append(tp)
            live[("ftp", t)] = banks

        def ff_out(t):
            fg = work2.tile([P, 2048], BF16, tag="fg", align_bytes=64)
            gw = fg[:].bitcast(F32).rearrange("p (g r u) -> p g r u", g=4, u=2)
            for gp in range(2):
                nc.scalar.copy(out=gw[:, 2 * gp:2 * gp + 2], in_=live[("ftp", t)][gp][:].rearrange("p g u r -> p g r u"))
            live[("fg", t)] = fg

        def ff_quantise(t):
            nc.vector.quantize_mx(out=fc[:, t, :].bitcast(FP8X4), scales=fs[:, t, :], in_=live[("fg", t)][:])

        def residual(t):
            tgtb = work2.tile([P, D], F32, tag="tgtb")
            nc.vector.tensor_tensor(out=tgtb[:], in0=raws[("t", t // 2)][:, t % 2, :], in1=b2bc[:], op=ALU.add)
            live[("tgtb", t)] = tgtb

        def stage1_mm(t):
            banks = []
            for h in range(2):
                mm = psum.tile([P, 512], F32, tag="mm")
                for g in range(4):
                    nc.tensor.matmul_mx(
                        out=mm[:],
                        lhsT=fc[:, t, g * 128:(g + 1) * 128].bitcast(FP8X4),
                        lhsT_scale=fs[:, t, g * 128:(g + 1) * 128],
                        rhs=w2c[:, g, 512 * h:512 * h + 512].bitcast(FP8X4),
                        rhs_scale=w2s[:, g, 512 * h:512 * h + 512],
                        start=(g == 0),
                        stop=(g == 3),
                    )
                banks.append(mm)
            live[("mm", t)] = banks

        def stage1_out(t):
            u = work4.tile([P, D], F32, tag="u")
            ssum = small.tile([P, 2], F32, tag="ssum")
            tgtb = live[("tgtb", t)]
            for h in range(2):
                u_half = u[:, 512 * h:512 * h + 512]
                if t < SCALAR_NORM_FROM:
                    u_half = u_half.rearrange("p (t m) -> p m t", t=4)
                else:
                    u_half = u_half.rearrange("p (m t) -> p m t", t=4)
                nc.vector.scalar_tensor_tensor(
                    out=u_half,
                    in0=live[("mm", t)][h][:].rearrange("p (m t) -> p m t", t=4),
                    scalar=0.0,
                    in1=tgtb[:, 512 * h:512 * h + 512].rearrange("p (m t) -> p m t", t=4),
                    op0=ALU.add,
                    op1=ALU.add,
                    accum_out=ssum[:, h:h + 1],
                )
            negmean = small.tile([P, 1], F32, tag="negmean")
            nc.vector.tensor_scalar(
                out=negmean[:], in0=ssum[:, 0:1], scalar1=ssum[:, 1:2], scalar2=-1.0 / D,
                op0=ALU.add, op1=ALU.mult,
            )
            live[("u", t)] = u
            live[("negmean", t)] = negmean

        def variance(t):
            sq = work1.tile([P, D], BF16, tag="sq")
            ssq = small.tile([P, 1], F32, tag="ssq")
            nc.scalar.activation(
                out=sq[:], in_=live[("u", t)][:], func=ACT.Square, bias=live[("negmean", t)][:], scale=1.0,
                accum_out=ssq[:],
            )
            std = small.tile([P, 1], F32, tag="std")
            nc.scalar.activation(out=std[:], in_=ssq[:], func=ACT.Sqrt, bias=eps[:], scale=1.0 / D)
            live[("std", t)] = std

        def norm_factors(t):
            rstd = small.tile([P, 1], F32, tag="rstd")
            nc.vector.reciprocal(out=rstd[:], in_=live[("std", t)][:])
            nbias = small.tile([P, 1], F32, tag="nbias")
            nc.scalar.activation(out=nbias[:], in_=live[("negmean", t)][:], func=ACT.Copy, scale=rstd[:, 0:1])
            live[("nbias", t)] = nbias
            if t < SCALAR_NORM_FROM:
                dg = work4.tile([P, P], F32, tag="dg")
                nc.scalar.activation(out=dg[:], in_=perm[:], func=ACT.Copy, scale=rstd[:, 0:1])
                live[("dg", t)] = dg
            else:
                zp = work2.tile([P, D], F32, tag="zp")
                nc.scalar.activation(
                    out=zp[:].rearrange("p (c t m) -> p c m t", c=2, t=4),
                    in_=live[("u", t)][:].rearrange("p (c m t) -> p c m t", c=2, t=4),
                    func=ACT.Identity, bias=nbias[:], scale=rstd[:, 0:1],
                )
                live[("zp", t)] = zp

        def norm_flip(t):
            banks = []
            for bk in range(2):
                zt = psum.tile([P, 4, P], F32, tag="zt")
                for q in range(4):
                    pl = 4 * bk + q
                    if t < SCALAR_NORM_FROM:
                        nc.tensor.matmul(
                            out=zt[:, q, :], lhsT=live[("u", t)][:, pl * 128:(pl + 1) * 128], rhs=live[("dg", t)][:],
                            start=True, stop=False,
                        )
                        nc.tensor.matmul(
                            out=zt[:, q, :], lhsT=live[("nbias", t)][:, 0:1].to_broadcast([P, P]), rhs=perm[:],
                            is_transpose=True, start=False, stop=True,
                        )
                    else:
                        nc.tensor.transpose(zt[:, q, :], live[("zp", t)][:, pl * 128:(pl + 1) * 128], perm[:])
                banks.append(zt)
            live[("zt", t)] = banks

        def gain_shift(t):
            hTp = work2.tile([P, 8, P], BF16, tag="hTp")
            for pl in range(8):
                nc.scalar.activation(
                    out=hTp[:, pl, :], in_=live[("zt", t)][pl // 4][:, pl % 4, :],
                    func=ACT.Identity, bias=be3T[:, pl:pl + 1], scale=g3T[:, pl:pl + 1],
                )
            live[("hTp", t)] = hTp

        def h_regroup(t):
            hg = work2.tile([P, 1024], BF16, tag="hg", align_bytes=64)
            nc.vector.tensor_copy(
                out=hg[:].rearrange("p (c a i t) -> p c a t i", c=2, i=4, t=4),
                in_=live[("hTp", t)][:].rearrange("p (c t) (a i) -> p c a t i", c=2, i=4),
            )
            live[("hg", t)] = hg

        def h_quantise(t):
            nc.vector.quantize_mx(out=hc[:, t, :].bitcast(FP8X4), scales=hs[:, t, :], in_=live[("hg", t)][:])

        def stage2_mm(i):
            banks = []
            for hh in range(2):
                s2 = psum.tile([P, 512], F32, tag="s2")
                for kq in range(4):
                    kk = 4 * hh + kq
                    for c in range(2):
                        xq = live[("c", 2 * i + c)]
                        nc.tensor.matmul_mx(
                            out=s2[:, kq * 128:(kq + 1) * 128],
                            lhsT=xq[0][:, kk * 128:(kk + 1) * 128].bitcast(FP8X4),
                            lhsT_scale=xq[1][:, kk * 128:(kk + 1) * 128],
                            rhs=hc[:, i, c * 128:(c + 1) * 128].bitcast(FP8X4),
                            rhs_scale=hs[:, i, c * 128:(c + 1) * 128],
                            start=(c == 0),
                            stop=(c == 1),
                        )
                banks.append(s2)
            live[("s2", i)] = banks

        def stage2_pick(i):
            oT = work2.tile([P, P], F32, tag="oT")
            for hh in range(2):
                nc.scalar.copy(
                    out=oT[:].rearrange("p (b k) -> p b k", k=8)[:, :, 4 * hh:4 * hh + 4],
                    in_=live[("s2", i)][hh][:].rearrange("p (x y) -> p x y", y=16)[:, 4 * hh:4 * hh + 28:9, :].rearrange("p q b -> p b q"),
                )
            ot = psum.tile([P, P], F32, tag="tp")
            nc.tensor.matmul(out=ot[:], lhsT=oT[:], rhs=ident[:], is_transpose=True, start=True, stop=False)
            nc.tensor.matmul(out=ot[:], lhsT=bexp[:, i, :], rhs=ident[:], is_transpose=True, start=False, stop=True)
            live[("ot", i)] = ot

        def stage2_store(i):
            nc.scalar.copy(out=o_all[:, i * 128:(i + 1) * 128], in_=live[("ot", i)][:])
            nc.scalar.dma_start(out=outv[:, i * 128:(i + 1) * 128], in_=o_all[:, i * 128:(i + 1) * 128])

        b2_spread()
        for m in range(n_ticks):
            key = plan[m] if m < len(plan) else None
            prev = plan[m - 1] if 0 < m <= len(plan) else None
            if tile_at(m, LAG["FT"]) >= 0:
                ff_transpose(tile_at(m, LAG["FT"]))
            for i in range(NT):
                if o_tick[i] == m:
                    stage2_mm(i)
            if tile_at(m, LAG["E"]) >= 0:
                stage1_out(tile_at(m, LAG["E"]))
            if tile_at(m, LAG["SQ"]) >= 0:
                variance(tile_at(m, LAG["SQ"]))
            if key is not None:
                regroup_s(key, V_BLOCKS, V_BLOCKS + S_FIRST)
            for i in range(NT):
                if o_tick[i] + LAG["OE"] == m:
                    stage2_pick(i)
            if tile_at(m, LAG["R"]) >= 0:
                norm_factors(tile_at(m, LAG["R"]))
                norm_flip(tile_at(m, LAG["R"]))
            if key is not None:
                regroup_v(key, V_BLOCKS)
            if prev is not None:
                quantise_bulk(prev)
            if tile_at(m, LAG["MM"]) >= 0:
                stage1_mm(tile_at(m, LAG["MM"]))
            if tile_at(m, LAG["FE"]) >= 0:
                ff_out(tile_at(m, LAG["FE"]))
            if tile_at(m, LAG["T"]) >= 0:
                residual(tile_at(m, LAG["T"]))
            if m == CONST_TICK:
                consts()
            if tile_at(m, LAG["ZE"]) >= 0:
                gain_shift(tile_at(m, LAG["ZE"]))
            if tile_at(m, LAG["FQ"]) >= 0:
                ff_quantise(tile_at(m, LAG["FQ"]))
            if tile_at(m, LAG["HR"]) >= 0:
                h_regroup(tile_at(m, LAG["HR"]))
            if key is not None:
                regroup_s(key, V_BLOCKS + S_FIRST, 8)
            for i in range(NT):
                if o_tick[i] + LAG["OC"] == m:
                    stage2_store(i)
            if tile_at(m, LAG["HQ"]) >= 0:
                h_quantise(tile_at(m, LAG["HQ"]))
